import numpy as np
import ml_dtypes


def mxq(x, axis, fmt="e4m3"):
    dtype, down = {"e4m3": (ml_dtypes.float8_e4m3fn, 7), "e5m2": (ml_dtypes.float8_e5m2, 14)}[fmt]
    v = np.moveaxis(np.asarray(x, np.float32).astype(ml_dtypes.bfloat16).astype(np.float64), axis, -1)
    blocks = v.reshape(v.shape[:-1] + (-1, 32))
    amax = np.abs(blocks).max(-1, keepdims=True)
    byte = np.maximum(np.where(amax > 0, np.frexp(amax)[1] - 1 + 127, 0) - down, 1)
    scale = np.exp2(byte - 127.0)
    codes = (blocks / scale).astype(np.float32).astype(dtype).astype(np.float64)
    return np.moveaxis((codes * scale).reshape(v.shape), -1, axis)


WIDE = False


def mx_kscale(k):
    if not WIDE:
        return np.ones(k)
    levels = np.array([10, -10, 5, -5, 0])
    if k % 512:
        return np.exp2(np.random.permutation(np.resize(levels, k // 32))).repeat(32)
    a = np.empty((k // 512, 16))
    for p in range(k // 512):
        a[p, :8] = np.random.permutation(np.resize(levels, 8))
        for g in range(8):
            far = levels[np.abs(levels - a[p, g]) >= 10]
            a[p, g + 8] = far[np.random.randint(len(far))]
    return np.exp2(a.ravel()).repeat(32)


BF16 = ml_dtypes.bfloat16


def bf(x):
    return np.asarray(x, np.float32).astype(BF16)


def f64(x):
    return np.asarray(x).astype(np.float64)


B, T, KA, KT, DIM, NH, HD, E = 16, 512, 256, 256, 512, 1, 128, 8
ROPE_BASE = 10000.0


def rope_cos_sin(L, hd):
    inv_freq = 1.0 / (ROPE_BASE ** (f64(np.arange(0, hd, 2)) / hd))
    freqs = f64(np.arange(L))[:, None] * inv_freq[None, :]
    emb = np.concatenate([freqs, freqs], axis=-1)
    return np.cos(emb), np.sin(emb)


def rotate_half(x):
    x1 = x[..., 0::2]
    x2 = x[..., 1::2]
    return np.stack((-x2, x1), axis=-1).reshape(x.shape)


def rope(t, cos, sin):
    return t * cos[None, None] + rotate_half(t) * sin[None, None]


def heads(t):
    return t.reshape(B, -1, NH, HD).transpose(0, 2, 1, 3)


def setup_inputs():
    s = mx_kscale(DIM)
    c = 1.2 / np.sqrt(DIM)
    return {"x": bf(np.random.standard_normal((B, T, DIM)) * s),
            "W_qa": bf(np.random.standard_normal((NH * HD, DIM)) * c / s[None, :]),
            "b_qa": bf(np.random.standard_normal(NH * HD) * 0.3),
            "W_qt": bf(np.random.standard_normal((NH * HD, DIM)) * c / s[None, :]),
            "b_qt": bf(np.random.standard_normal(NH * HD) * 0.3)}


def reference(x, W_qa, b_qa, W_qt, b_qt):
    xq = mxq(f64(x), 2, "e4m3")
    q_a = heads((xq @ mxq(f64(W_qa), 1, "e4m3").T) + f64(b_qa))
    q_t = heads((xq @ mxq(f64(W_qt), 1, "e4m3").T) + f64(b_qt))
    cos_m, sin_m = rope_cos_sin(T, HD)
    return rope(q_a, cos_m, sin_m), rope(q_t, cos_m, sin_m)

@@ -1,0 +1,228 @@
+import math
+from contextlib import ExitStack
+
+import concourse.mybir as mybir
+from concourse.masks import make_identity
+
+F32 = mybir.dt.float32
+BF16 = mybir.dt.bfloat16
+I32 = mybir.dt.int32
+U32 = mybir.dt.uint32
+U8 = mybir.dt.uint8
+FP8X4 = mybir.dt.float8_e4m3fn_x4
+ALU = mybir.AluOpType
+ACT = mybir.ActivationFunctionType
+
+P = 128
+NB = 16
+T = 512
+K = 512
+D = 128
+TI = 4
+GSET = ()
+
+FLOPS = 2 * NB * T * K * 2 * D
+
+
+def tile_l1regressionmoeactionhead_pa_t_kernel(tc, x, W_qa, b_qa, W_qt, b_qt, out_0, out_1):
+    nc = tc.nc
+    outs = (out_0, out_1)
+    with ExitStack() as ctx:
+        const = ctx.enter_context(tc.tile_pool(name="const", bufs=1))
+        xin = ctx.enter_context(tc.tile_pool(name="xin", bufs=NB))
+        grp = ctx.enter_context(tc.tile_pool(name="grp", bufs=3))
+        cod = ctx.enter_context(tc.tile_pool(name="cod", bufs=3))
+        prod = ctx.enter_context(tc.tile_pool(name="prod", bufs=4))
+        qsb = ctx.enter_context(tc.tile_pool(name="qsb", bufs=2)) if GSET else None
+        ost = ctx.enter_context(tc.tile_pool(name="ost", bufs=4))
+        psx = ctx.enter_context(tc.psum_pool(name="psx", bufs=2))
+        psp = ctx.enter_context(tc.psum_pool(name="psp", bufs=4))
+        pso = ctx.enter_context(tc.psum_pool(name="pso", bufs=2))
+        ctx.enter_context(tc.manual_schedule())
+
+        w_sb = []
+        for w, W in enumerate((W_qa, W_qt)):
+            wt = const.tile([P, K], BF16, name="w_sb%d" % w)
+            nc.scalar.dma_start(out=wt[:], in_=W)
+            w_sb.append(wt)
+        brow = const.tile([P, D], BF16, name="brow")
+        nc.gpsimd.memset(brow[:], 0.0)
+        nc.scalar.dma_start(out=brow[0:1, :], in_=b_qa.unsqueeze(0))
+        nc.scalar.dma_start(out=brow[1:2, :], in_=b_qt.unsqueeze(0))
+        x_sb = []
+        for n in range(NB):
+            xt_in = xin.tile([P, TI * K], BF16, name="x_sb")
+            nc.sync.dma_start(out=xt_in[:], in_=x[n].rearrange("(p i) k -> p (i k)", i=TI))
+            x_sb.append(xt_in)
+
+        tp = const.tile([P, P], I32, name="tp")
+        nc.gpsimd.iota(tp[:], pattern=[[TI, P]], base=0, channel_multiplier=0)
+        ident = const.tile([P, P], F32, name="ident")
+        make_identity(nc, ident[:])
+
+        ratio = 10000.0 ** (-1.0 / 64.0)
+        f2 = const.tile([P, 2, D], F32, name="f2")
+        nc.vector.memset(f2[:, 0, 0:1], 1.0)
+        nc.vector.tensor_scalar_mul(out=f2[:, 0, 0:1], in0=f2[:, 0, 0:1], scalar1=1.0 / (2.0 * math.pi))
+        junk = const.tile([P, 1], F32, name="junk")
+        nc.scalar.activation(out=junk[:], in_=f2[:, 0, 0:1], func=ACT.Sin)
+        for step in range(7):
+            width = 2**step
+            nc.vector.tensor_scalar_mul(
+                out=f2[:, 0, width : 2 * width], in0=f2[:, 0, 0:width],
+                scalar1=(ratio**width if step < 6 else 1.0),
+            )
+        fc_v = f2[:, 0, :].rearrange("p (i e) -> p i e", e=2)
+        fs_v = f2[:, 1, :].rearrange("p (i e) -> p i e", e=2)
+        nc.vector.tensor_copy(out=fs_v[:, :, 0], in_=fc_v[:, :, 1])
+        nc.vector.tensor_scalar_mul(out=fs_v[:, :, 1], in0=fc_v[:, :, 0], scalar1=-1.0)
+        setup_f = pso.tile([P, 2, P], F32, name="setup_f", tag="o")
+        nc.tensor.transpose(setup_f[:, 0, :], f2[:, 0, :], ident[:])
+        nc.tensor.transpose(setup_f[:, 1, :], f2[:, 1, :], ident[:])
+        tf = const.tile([P, T], F32, name="tf")
+        for i in range(TI):
+            nc.vector.tensor_scalar_add(out=tf[:, P * i : P * i + P], in0=tp[:], scalar1=float(i))
+        cstf = const.tile([P, 2], F32, name="cstf")
+        nc.vector.tensor_copy(out=cstf[:], in_=setup_f[:, :, 0])
+
+        turns = const.tile([P, T], F32, name="turns")
+        whole = const.tile([P, 2, T], I32, name="whole")
+        frac = const.tile([P, 2, T], F32, name="frac")
+        tab = const.tile([P, 2, T], F32, name="tab")
+        nc.vector.tensor_scalar(
+            out=turns[:], in0=tf[:], scalar1=cstf[:, 0:1], scalar2=0.25, op0=ALU.mult, op1=ALU.add
+        )
+        nc.vector.tensor_copy(out=whole[:, 0, :], in_=turns[:])
+        nc.vector.tensor_tensor(out=frac[:, 0, :], in0=turns[:], in1=whole[:, 0, :], op=ALU.subtract)
+
+        wt_ps = psx.tile([P, 4, P], F32, name="wt_ps", tag="xt")
+        for w in range(2):
+            ww = w_sb[w][:].bitcast(F32)
+            for u in range(2):
+                nc.tensor.transpose(wt_ps[:, 2 * w + u, :], ww[:, u : K // 2 : 2], ident[:])
+        wg = const.tile([P, 2 * D * 4], BF16, name="wg", align_bytes=64)
+        nc.scalar.copy(
+            out=wg[:].bitcast(F32).rearrange("p (w d u) -> p w d u", w=2, u=2),
+            in_=wt_ps[:].rearrange("p (w u) d -> p w d u", u=2),
+        )
+
+        xg = {}
+        xq = {}
+        pp = {}
+        ab = {}
+        osb = {}
+
+        def xpose(n, second_on_vector=False):
+            g = grp.tile([P, TI * K], BF16, name="xg", align_bytes=64)
+            gw = g[:].bitcast(F32)
+            xw = x_sb[n][:].bitcast(F32)
+            for h in range(2):
+                xt = psx.tile([P, 2, 2, P], F32, name="xt", tag="xt")
+                for i2 in range(2):
+                    for u in range(2):
+                        c0 = (2 * h + i2) * 256
+                        nc.tensor.transpose(xt[:, i2, u, :], xw[:, c0 + u : c0 + 256 : 2], ident[:])
+                dst = gw[:, 512 * h : 512 * h + 512].rearrange("p (i t u) -> p i t u", i=2, u=2)
+                src = xt[:].rearrange("p i u t -> p i t u")
+                if h == 1 and second_on_vector:
+                    nc.vector.tensor_copy(out=dst, in_=src)
+                else:
+                    nc.scalar.copy(out=dst, in_=src)
+            xg[n] = g
+
+        def quant(n):
+            c = cod.tile([P, T], U32, name="xc", align_bytes=64)
+            s = cod.tile([P, T], U8, name="xs", align_bytes=64)
+            nc.vector.quantize_mx(out=c[:].bitcast(FP8X4), scales=s[:], in_=xg[n][:])
+            xq[n] = (c, s)
+
+        def mx(n):
+            c, s = xq[n]
+            for w in range(2):
+                acc = psp.tile([P, T], F32, name="acc")
+                nc.tensor.matmul_mx(
+                    out=acc[:],
+                    lhsT=wc[:, D * w : D * w + D].bitcast(FP8X4),
+                    lhsT_scale=ws[:, D * w : D * w + D],
+                    rhs=c[:].bitcast(FP8X4),
+                    rhs_scale=s[:],
+                    start=True,
+                    stop=True,
+                )
+                pp[(n, w)] = acc
+
+        def rope(n):
+            if n in GSET:
+                q = qsb.tile([P, T], F32, name="q")
+                nc.scalar.activation(out=q[:], in_=pp[(n, 1)][:], func=ACT.Identity, bias=cstb[:, 1:2])
+                for j in range(2):
+                    t = prod.tile([P, T], F32, name="prod%d" % j)
+                    nc.gpsimd.tensor_tensor(out=t[:], in0=q[:], in1=tab[:, j, :], op=ALU.mult)
+                    ab[(n, 1, j)] = t
+            for w in range(1 if n in GSET else 2):
+                for j in range(2):
+                    t = prod.tile([P, T], F32, name="prod%d" % j)
+                    nc.vector.scalar_tensor_tensor(
+                        out=t[:], in0=pp[(n, w)][:], scalar=cstb[:, w : w + 1], in1=tab[:, j, :],
+                        op0=ALU.add, op1=ALU.mult,
+                    )
+                    ab[(n, w, j)] = t
+
+        def opose(n, w):
+            if w == 0:
+                osb[n] = ost.tile([P, 2, TI * D], F32, name="o_sb")
+            o_sb = osb[n]
+            o = pso.tile([P, TI, D], F32, name="o", tag="o")
+            for i in range(TI):
+                nc.tensor.matmul(
+                    o[:, i, :], lhsT=ab[(n, w, 0)][:, P * i : P * i + P], rhs=ident[:],
+                    is_transpose=True, start=True, stop=False,
+                )
+                nc.tensor.matmul(
+                    o[:, i, :], lhsT=ab[(n, w, 1)][:, P * i : P * i + P], rhs=perm[:],
+                    is_transpose=True, start=False, stop=True,
+                )
+            nc.scalar.copy(out=o_sb[:, w, :], in_=o[:].rearrange("p i d -> p (i d)"))
+            nc.sync.dma_start(out=outs[w][n, 0].rearrange("(p i) d -> p (i d)", i=TI), in_=o_sb[:, w, :])
+
+        xpose(0)
+        perm = const.tile([P, P], F32, name="perm")
+        ident_v = ident[:].rearrange("p (i e) -> p i e", e=2)
+        perm_v = perm[:].rearrange("p (i e) -> p i e", e=2)
+        nc.gpsimd.tensor_copy(out=perm_v[:, :, 0], in_=ident_v[:, :, 1])
+        nc.gpsimd.tensor_copy(out=perm_v[:, :, 1], in_=ident_v[:, :, 0])
+        brow_f = const.tile([P, D], F32, name="brow_f")
+        nc.gpsimd.tensor_copy(out=brow_f[:], in_=brow[:])
+        nc.vector.tensor_scalar_mul(out=whole[:, 1, :], in0=tf[:], scalar1=cstf[:, 1:2])
+        nc.vector.scalar_tensor_tensor(
+            out=frac[:, 1, :], in0=tf[:], scalar=cstf[:, 1:2], in1=whole[:, 1, :],
+            op0=ALU.mult, op1=ALU.subtract,
+        )
+        wc = const.tile([P, 2 * D], U32, name="wc", align_bytes=64)
+        ws = const.tile([P, 2 * D], U8, name="ws", align_bytes=64)
+        nc.vector.quantize_mx(out=wc[:].bitcast(FP8X4), scales=ws[:], in_=wg[:])
+        quant(0)
+        xpose(1, second_on_vector=True)
+        setup_b = pso.tile([P, P], F32, name="setup_b", tag="o")
+        nc.tensor.transpose(setup_b[:], brow_f[:], ident[:])
+        nc.scalar.activation(out=tab[:, 0, :], in_=frac[:, 0, :], func=ACT.Sin, scale=2.0 * math.pi)
+        nc.scalar.activation(out=tab[:, 1, :], in_=frac[:, 1, :], func=ACT.Sin, scale=2.0 * math.pi)
+        mx(0)
+        cstb = const.tile([P, 2], F32, name="cstb")
+        nc.vector.tensor_copy(out=cstb[:], in_=setup_b[:, 0:2])
+        quant(1)
+        xpose(2)
+
+        for k in range(NB + 1):
+            if k + 1 < NB:
+                mx(k + 1)
+            if k < NB:
+                rope(k)
+            if k >= 1:
+                opose(k - 1, 0)
+            if k + 3 < NB:
+                xpose(k + 3)
+            if k >= 1:
+                opose(k - 1, 1)
+            if k + 2 < NB:
+                quant(k + 2)

@@ -18,8 +18,8 @@ NB = 16
 T = 512
 K = 512
 D = 128
+J = 64
 TI = 4
-GSET = ()
 
 FLOPS = 2 * NB * T * K * 2 * D
 
@@ -32,12 +32,12 @@ def tile_l1regressionmoeactionhead_pa_t_kernel(tc, x, W_qa, b_qa, W_qt, b_qt, ou
         xin = ctx.enter_context(tc.tile_pool(name="xin", bufs=NB))
         grp = ctx.enter_context(tc.tile_pool(name="grp", bufs=3))
         cod = ctx.enter_context(tc.tile_pool(name="cod", bufs=3))
-        prod = ctx.enter_context(tc.tile_pool(name="prod", bufs=4))
-        qsb = ctx.enter_context(tc.tile_pool(name="qsb", bufs=2)) if GSET else None
-        ost = ctx.enter_context(tc.tile_pool(name="ost", bufs=4))
+        qsb = ctx.enter_context(tc.tile_pool(name="qsb", bufs=4))
+        prod = ctx.enter_context(tc.tile_pool(name="prod", bufs=3))
+        ost = ctx.enter_context(tc.tile_pool(name="ost", bufs=6))
         psx = ctx.enter_context(tc.psum_pool(name="psx", bufs=2))
-        psp = ctx.enter_context(tc.psum_pool(name="psp", bufs=4))
-        pso = ctx.enter_context(tc.psum_pool(name="pso", bufs=2))
+        psp = ctx.enter_context(tc.psum_pool(name="psp", bufs=2))
+        pso = ctx.enter_context(tc.psum_pool(name="pso", bufs=4))
         ctx.enter_context(tc.manual_schedule())
 
         w_sb = []
@@ -55,45 +55,42 @@ def tile_l1regressionmoeactionhead_pa_t_kernel(tc, x, W_qa, b_qa, W_qt, b_qt, ou
             nc.sync.dma_start(out=xt_in[:], in_=x[n].rearrange("(p i) k -> p (i k)", i=TI))
             x_sb.append(xt_in)
 
-        tp = const.tile([P, P], I32, name="tp")
-        nc.gpsimd.iota(tp[:], pattern=[[TI, P]], base=0, channel_multiplier=0)
+        tok = const.tile([P, TI], I32, name="tok")
+        nc.gpsimd.iota(tok[:], pattern=[[1, TI]], base=0, channel_multiplier=TI)
         ident = const.tile([P, P], F32, name="ident")
         make_identity(nc, ident[:])
+        brow_f = const.tile([P, D], F32, name="brow_f")
+        nc.gpsimd.tensor_copy(out=brow_f[:], in_=brow[:])
 
-        ratio = 10000.0 ** (-1.0 / 64.0)
-        f2 = const.tile([P, 2, D], F32, name="f2")
-        nc.vector.memset(f2[:, 0, 0:1], 1.0)
-        nc.vector.tensor_scalar_mul(out=f2[:, 0, 0:1], in0=f2[:, 0, 0:1], scalar1=1.0 / (2.0 * math.pi))
+        ratio = 10000.0 ** (-1.0 / J)
+        freq = const.tile([P, 2, J], F32, name="freq")
+        nc.vector.memset(freq[:, 0, 0:1], 1.0)
+        nc.vector.tensor_scalar_mul(out=freq[:, 0, 0:1], in0=freq[:, 0, 0:1], scalar1=1.0 / (2.0 * math.pi))
         junk = const.tile([P, 1], F32, name="junk")
-        nc.scalar.activation(out=junk[:], in_=f2[:, 0, 0:1], func=ACT.Sin)
-        for step in range(7):
+        nc.scalar.activation(out=junk[:], in_=freq[:, 0, 0:1], func=ACT.Sin)
+        for step in range(6):
             width = 2**step
             nc.vector.tensor_scalar_mul(
-                out=f2[:, 0, width : 2 * width], in0=f2[:, 0, 0:width],
-                scalar1=(ratio**width if step < 6 else 1.0),
+                out=freq[:, 0, width : 2 * width], in0=freq[:, 0, 0:width], scalar1=ratio**width
             )
-        fc_v = f2[:, 0, :].rearrange("p (i e) -> p i e", e=2)
-        fs_v = f2[:, 1, :].rearrange("p (i e) -> p i e", e=2)
-        nc.vector.tensor_copy(out=fs_v[:, :, 0], in_=fc_v[:, :, 1])
-        nc.vector.tensor_scalar_mul(out=fs_v[:, :, 1], in0=fc_v[:, :, 0], scalar1=-1.0)
-        setup_f = pso.tile([P, 2, P], F32, name="setup_f", tag="o")
-        nc.tensor.transpose(setup_f[:, 0, :], f2[:, 0, :], ident[:])
-        nc.tensor.transpose(setup_f[:, 1, :], f2[:, 1, :], ident[:])
-        tf = const.tile([P, T], F32, name="tf")
-        for i in range(TI):
-            nc.vector.tensor_scalar_add(out=tf[:, P * i : P * i + P], in0=tp[:], scalar1=float(i))
-        cstf = const.tile([P, 2], F32, name="cstf")
-        nc.vector.tensor_copy(out=cstf[:], in_=setup_f[:, :, 0])
+        pair = freq[:].rearrange("p s (c e) -> p s c e", e=2)
+        nc.vector.tensor_scalar_mul(out=pair[:, 1, :, 0], in0=pair[:, 0, :, 0], scalar1=-1.0)
+        nc.vector.tensor_copy(out=pair[:, 1, :, 1], in_=pair[:, 0, :, 1])
+        tok_f = const.tile([P, TI], F32, name="tok_f")
+        nc.vector.tensor_copy(out=tok_f[:], in_=tok[:])
 
-        turns = const.tile([P, T], F32, name="turns")
-        whole = const.tile([P, 2, T], I32, name="whole")
-        frac = const.tile([P, 2, T], F32, name="frac")
-        tab = const.tile([P, 2, T], F32, name="tab")
-        nc.vector.tensor_scalar(
-            out=turns[:], in0=tf[:], scalar1=cstf[:, 0:1], scalar2=0.25, op0=ALU.mult, op1=ALU.add
+        turns = const.tile([P, 2, TI, J], F32, name="turns")
+        whole = const.tile([P, 2, TI, J], I32, name="whole")
+        frac = const.tile([P, 2, TI, J], F32, name="frac")
+        tab = const.tile([P, 2, TI, J], F32, name="tab")
+        for i in range(TI):
+            nc.vector.tensor_scalar_mul(out=turns[:, :, i, :], in0=freq[:], scalar1=tok_f[:, i : i + 1])
+        nc.vector.tensor_scalar_add(out=whole[:, 0], in0=turns[:, 0], scalar1=0.25)
+        nc.vector.tensor_copy(out=whole[:, 1], in_=turns[:, 1])
+        nc.vector.scalar_tensor_tensor(
+            out=frac[:, 0], in0=turns[:, 0], scalar=0.25, in1=whole[:, 0], op0=ALU.add, op1=ALU.subtract
         )
-        nc.vector.tensor_copy(out=whole[:, 0, :], in_=turns[:])
-        nc.vector.tensor_tensor(out=frac[:, 0, :], in0=turns[:], in1=whole[:, 0, :], op=ALU.subtract)
+        nc.vector.tensor_tensor(out=frac[:, 1], in0=turns[:, 1], in1=whole[:, 1], op=ALU.subtract)
 
         wt_ps = psx.tile([P, 4, P], F32, name="wt_ps", tag="xt")
         for w in range(2):
@@ -109,8 +106,8 @@ def tile_l1regressionmoeactionhead_pa_t_kernel(tc, x, W_qa, b_qa, W_qt, b_qt, ou
         xg = {}
         xq = {}
         pp = {}
-        ab = {}
-        osb = {}
+        qq = {}
+        oo = {}
 
         def xpose(n, second_on_vector=False):
             g = grp.tile([P, TI * K], BF16, name="xg", align_bytes=64)
@@ -151,78 +148,58 @@ def tile_l1regressionmoeactionhead_pa_t_kernel(tc, x, W_qa, b_qa, W_qt, b_qt, ou
                 )
                 pp[(n, w)] = acc
 
-        def rope(n):
-            if n in GSET:
+        def biased(n):
+            for w in range(2):
                 q = qsb.tile([P, T], F32, name="q")
-                nc.scalar.activation(out=q[:], in_=pp[(n, 1)][:], func=ACT.Identity, bias=cstb[:, 1:2])
-                for j in range(2):
-                    t = prod.tile([P, T], F32, name="prod%d" % j)
-                    nc.gpsimd.tensor_tensor(out=t[:], in0=q[:], in1=tab[:, j, :], op=ALU.mult)
-                    ab[(n, 1, j)] = t
-            for w in range(1 if n in GSET else 2):
-                for j in range(2):
-                    t = prod.tile([P, T], F32, name="prod%d" % j)
-                    nc.vector.scalar_tensor_tensor(
-                        out=t[:], in0=pp[(n, w)][:], scalar=cstb[:, w : w + 1], in1=tab[:, j, :],
-                        op0=ALU.add, op1=ALU.mult,
-                    )
-                    ab[(n, w, j)] = t
+                nc.scalar.activation(out=q[:], in_=pp[(n, w)][:], func=ACT.Identity, bias=cstb[:, w : w + 1])
+                qq[(n, w)] = q
 
         def opose(n, w):
-            if w == 0:
-                osb[n] = ost.tile([P, 2, TI * D], F32, name="o_sb")
-            o_sb = osb[n]
             o = pso.tile([P, TI, D], F32, name="o", tag="o")
             for i in range(TI):
-                nc.tensor.matmul(
-                    o[:, i, :], lhsT=ab[(n, w, 0)][:, P * i : P * i + P], rhs=ident[:],
-                    is_transpose=True, start=True, stop=False,
-                )
-                nc.tensor.matmul(
-                    o[:, i, :], lhsT=ab[(n, w, 1)][:, P * i : P * i + P], rhs=perm[:],
-                    is_transpose=True, start=False, stop=True,
-                )
-            nc.scalar.copy(out=o_sb[:, w, :], in_=o[:].rearrange("p i d -> p (i d)"))
-            nc.sync.dma_start(out=outs[w][n, 0].rearrange("(p i) d -> p (i d)", i=TI), in_=o_sb[:, w, :])
+                nc.tensor.transpose(o[:, i, :], qq[(n, w)][:, P * i : P * i + P], ident[:])
+            oo[(n, w)] = o
 
-        xpose(0)
-        perm = const.tile([P, P], F32, name="perm")
-        ident_v = ident[:].rearrange("p (i e) -> p i e", e=2)
-        perm_v = perm[:].rearrange("p (i e) -> p i e", e=2)
-        nc.gpsimd.tensor_copy(out=perm_v[:, :, 0], in_=ident_v[:, :, 1])
-        nc.gpsimd.tensor_copy(out=perm_v[:, :, 1], in_=ident_v[:, :, 0])
-        brow_f = const.tile([P, D], F32, name="brow_f")
-        nc.gpsimd.tensor_copy(out=brow_f[:], in_=brow[:])
-        nc.vector.tensor_scalar_mul(out=whole[:, 1, :], in0=tf[:], scalar1=cstf[:, 1:2])
-        nc.vector.scalar_tensor_tensor(
-            out=frac[:, 1, :], in0=tf[:], scalar=cstf[:, 1:2], in1=whole[:, 1, :],
-            op0=ALU.mult, op1=ALU.subtract,
-        )
+        def rope(n, w):
+            o = oo[(n, w)][:].rearrange("p i (h c e) -> p i h c e", h=2, e=2)
+            cos = tab[:, 0].rearrange("p i (c e) -> p i c e", e=2).unsqueeze(2).to_broadcast([P, TI, 2, J // 2, 2])
+            sin = tab[:, 1].rearrange("p i (c e) -> p i c e", e=2).unsqueeze(2).to_broadcast([P, TI, 2, J // 2, 2])
+            a = prod.tile([P, T], F32, name="prod_a")
+            b = prod.tile([P, T], F32, name="prod_b")
+            view = "p (i h c e) -> p i h c e"
+            nc.vector.tensor_tensor(out=a[:].rearrange(view, i=TI, h=2, e=2), in0=o, in1=cos, op=ALU.mult)
+            nc.vector.tensor_tensor(
+                out=b[:].rearrange(view, i=TI, h=2, e=2), in0=o[:, :, :, :, ::-1], in1=sin, op=ALU.mult
+            )
+            o_sb = ost.tile([P, TI * D], F32, name="o_sb")
+            nc.gpsimd.tensor_tensor(out=o_sb[:], in0=a[:], in1=b[:], op=ALU.add)
+            nc.sync.dma_start(out=outs[w][n, 0].rearrange("(p i) d -> p (i d)", i=TI), in_=o_sb[:])
+
+        xpose(0, second_on_vector=True)
         wc = const.tile([P, 2 * D], U32, name="wc", align_bytes=64)
         ws = const.tile([P, 2 * D], U8, name="ws", align_bytes=64)
         nc.vector.quantize_mx(out=wc[:].bitcast(FP8X4), scales=ws[:], in_=wg[:])
         quant(0)
-        xpose(1, second_on_vector=True)
         setup_b = pso.tile([P, P], F32, name="setup_b", tag="o")
         nc.tensor.transpose(setup_b[:], brow_f[:], ident[:])
-        nc.scalar.activation(out=tab[:, 0, :], in_=frac[:, 0, :], func=ACT.Sin, scale=2.0 * math.pi)
-        nc.scalar.activation(out=tab[:, 1, :], in_=frac[:, 1, :], func=ACT.Sin, scale=2.0 * math.pi)
-        mx(0)
         cstb = const.tile([P, 2], F32, name="cstb")
         nc.vector.tensor_copy(out=cstb[:], in_=setup_b[:, 0:2])
+        nc.scalar.activation(out=tab[:], in_=frac[:], func=ACT.Sin, scale=2.0 * math.pi)
+        xpose(1, second_on_vector=True)
+        mx(0)
+        biased(0)
         quant(1)
         xpose(2)
 
-        for k in range(NB + 1):
+        for k in range(NB):
+            opose(k, 0)
+            opose(k, 1)
             if k + 1 < NB:
                 mx(k + 1)
-            if k < NB:
-                rope(k)
-            if k >= 1:
-                opose(k - 1, 0)
+                biased(k + 1)
             if k + 3 < NB:
                 xpose(k + 3)
-            if k >= 1:
-                opose(k - 1, 1)
+            rope(k, 0)
             if k + 2 < NB:
                 quant(k + 2)
+            rope(k, 1)

@@ -156,7 +156,8 @@ def tile_l1regressionmoeactionhead_pa_t_kernel(tc, x, W_qa, b_qa, W_qt, b_qt, ou
 
         def opose(n, w):
             o = pso.tile([P, TI, D], F32, name="o", tag="o")
-            for i in range(TI):
+            nc.tensor.matmul(o[:, 0, :], lhsT=qq[(n, w)][:, 0:P], rhs=ident[:], start=True, stop=True)
+            for i in range(1, TI):
                 nc.tensor.transpose(o[:, i, :], qq[(n, w)][:, P * i : P * i + P], ident[:])
             oo[(n, w)] = o
 

@@ -32,12 +32,14 @@ def tile_l1regressionmoeactionhead_pa_t_kernel(tc, x, W_qa, b_qa, W_qt, b_qt, ou
         xin = ctx.enter_context(tc.tile_pool(name="xin", bufs=NB))
         grp = ctx.enter_context(tc.tile_pool(name="grp", bufs=3))
         cod = ctx.enter_context(tc.tile_pool(name="cod", bufs=3))
-        qsb = ctx.enter_context(tc.tile_pool(name="qsb", bufs=4))
+        qsb = ctx.enter_context(tc.tile_pool(name="qsb", bufs=2))
         prod = ctx.enter_context(tc.tile_pool(name="prod", bufs=3))
         ost = ctx.enter_context(tc.tile_pool(name="ost", bufs=6))
         psx = ctx.enter_context(tc.psum_pool(name="psx", bufs=2))
-        psp = ctx.enter_context(tc.psum_pool(name="psp", bufs=2))
-        pso = ctx.enter_context(tc.psum_pool(name="pso", bufs=4))
+        ps0 = ctx.enter_context(tc.psum_pool(name="ps0", bufs=1))
+        ps1 = ctx.enter_context(tc.psum_pool(name="ps1", bufs=2))
+        pso = ctx.enter_context(tc.psum_pool(name="pso", bufs=2))
+        pss = ctx.enter_context(tc.psum_pool(name="pss", bufs=1))
         ctx.enter_context(tc.manual_schedule())
 
         w_sb = []
@@ -57,8 +59,15 @@ def tile_l1regressionmoeactionhead_pa_t_kernel(tc, x, W_qa, b_qa, W_qt, b_qt, ou
 
         tok = const.tile([P, TI], I32, name="tok")
         nc.gpsimd.iota(tok[:], pattern=[[1, TI]], base=0, channel_multiplier=TI)
+        tp = const.tile([P, P], I32, name="tp")
+        nc.gpsimd.iota(tp[:], pattern=[[TI, P]], base=0, channel_multiplier=0)
         ident = const.tile([P, P], F32, name="ident")
         make_identity(nc, ident[:])
+        perm = const.tile([P, P], F32, name="perm")
+        ident_v = ident[:].rearrange("p (i e) -> p i e", e=2)
+        perm_v = perm[:].rearrange("p (i e) -> p i e", e=2)
+        nc.gpsimd.tensor_copy(out=perm_v[:, :, 0], in_=ident_v[:, :, 1])
+        nc.gpsimd.tensor_copy(out=perm_v[:, :, 1], in_=ident_v[:, :, 0])
         brow_f = const.tile([P, D], F32, name="brow_f")
         nc.gpsimd.tensor_copy(out=brow_f[:], in_=brow[:])
 
@@ -92,6 +101,35 @@ def tile_l1regressionmoeactionhead_pa_t_kernel(tc, x, W_qa, b_qa, W_qt, b_qt, ou
         )
         nc.vector.tensor_tensor(out=frac[:, 1], in0=turns[:, 1], in1=whole[:, 1], op=ALU.subtract)
 
+        f2 = const.tile([P, 2, 2, J], F32, name="f2")
+        for h in range(2):
+            nc.vector.tensor_copy(out=f2[:, 0, h, :], in_=freq[:, 0, :])
+            fs_v = f2[:, 1, h, :].rearrange("p (c e) -> p c e", e=2)
+            nc.vector.tensor_copy(out=fs_v[:, :, 0], in_=pair[:, 0, :, 1])
+            nc.vector.tensor_scalar_mul(out=fs_v[:, :, 1], in0=pair[:, 0, :, 0], scalar1=-1.0)
+        setup_f = pso.tile([P, 2, P], F32, name="setup_f", tag="o")
+        for c in range(2):
+            nc.tensor.transpose(setup_f[:, c, :], f2[:, c].rearrange("p h j -> p (h j)"), ident[:])
+        cstf = const.tile([P, 2], F32, name="cstf")
+        nc.vector.tensor_copy(out=cstf[:], in_=setup_f[:, :, 0])
+        tf = const.tile([P, T], F32, name="tf")
+        for i in range(TI):
+            nc.vector.tensor_scalar_add(out=tf[:, P * i : P * i + P], in0=tp[:], scalar1=float(i))
+        fturns = const.tile([P, T], F32, name="fturns")
+        fwhole = const.tile([P, 2, T], I32, name="fwhole")
+        ffrac = const.tile([P, 2, T], F32, name="ffrac")
+        ftab = const.tile([P, 2, T], F32, name="ftab")
+        nc.vector.tensor_scalar(
+            out=fturns[:], in0=tf[:], scalar1=cstf[:, 0:1], scalar2=0.25, op0=ALU.mult, op1=ALU.add
+        )
+        nc.vector.tensor_scalar_mul(out=fwhole[:, 1, :], in0=tf[:], scalar1=cstf[:, 1:2])
+        nc.vector.tensor_copy(out=fwhole[:, 0, :], in_=fturns[:])
+        nc.vector.scalar_tensor_tensor(
+            out=ffrac[:, 1, :], in0=tf[:], scalar=cstf[:, 1:2], in1=fwhole[:, 1, :],
+            op0=ALU.mult, op1=ALU.subtract,
+        )
+        nc.vector.tensor_tensor(out=ffrac[:, 0, :], in0=fturns[:], in1=fwhole[:, 0, :], op=ALU.subtract)
+
         wt_ps = psx.tile([P, 4, P], F32, name="wt_ps", tag="xt")
         for w in range(2):
             ww = w_sb[w][:].bitcast(F32)
@@ -108,24 +146,24 @@ def tile_l1regressionmoeactionhead_pa_t_kernel(tc, x, W_qa, b_qa, W_qt, b_qt, ou
         pp = {}
         qq = {}
         oo = {}
+        ab = {}
 
-        def xpose(n, second_on_vector=False):
-            g = grp.tile([P, TI * K], BF16, name="xg", align_bytes=64)
-            gw = g[:].bitcast(F32)
+        def xpose(n, h, engine):
+            if h == 0:
+                xg[n] = grp.tile([P, TI * K], BF16, name="xg", align_bytes=64)
+            gw = xg[n][:].bitcast(F32)
             xw = x_sb[n][:].bitcast(F32)
-            for h in range(2):
-                xt = psx.tile([P, 2, 2, P], F32, name="xt", tag="xt")
-                for i2 in range(2):
-                    for u in range(2):
-                        c0 = (2 * h + i2) * 256
-                        nc.tensor.transpose(xt[:, i2, u, :], xw[:, c0 + u : c0 + 256 : 2], ident[:])
-                dst = gw[:, 512 * h : 512 * h + 512].rearrange("p (i t u) -> p i t u", i=2, u=2)
-                src = xt[:].rearrange("p i u t -> p i t u")
-                if h == 1 and second_on_vector:
-                    nc.vector.tensor_copy(out=dst, in_=src)
-                else:
-                    nc.scalar.copy(out=dst, in_=src)
-            xg[n] = g
+            xt = psx.tile([P, 2, 2, P], F32, name="xt", tag="xt")
+            for i2 in range(2):
+                for u in range(2):
+                    c0 = (2 * h + i2) * 256
+                    nc.tensor.transpose(xt[:, i2, u, :], xw[:, c0 + u : c0 + 256 : 2], ident[:])
+            dst = gw[:, 512 * h : 512 * h + 512].rearrange("p (i t u) -> p i t u", i=2, u=2)
+            src = xt[:].rearrange("p i u t -> p i t u")
+            if engine == "vector":
+                nc.vector.tensor_copy(out=dst, in_=src)
+            else:
+                nc.scalar.copy(out=dst, in_=src)
 
         def quant(n):
             c = cod.tile([P, T], U32, name="xc", align_bytes=64)
@@ -135,8 +173,8 @@ def tile_l1regressionmoeactionhead_pa_t_kernel(tc, x, W_qa, b_qa, W_qt, b_qt, ou
 
         def mx(n):
             c, s = xq[n]
-            for w in range(2):
-                acc = psp.tile([P, T], F32, name="acc")
+            for w, pool in ((1, ps1), (0, ps0)):
+                acc = pool.tile([P, T], F32, name="acc%d" % w)
                 nc.tensor.matmul_mx(
                     out=acc[:],
                     lhsT=wc[:, D * w : D * w + D].bitcast(FP8X4),
@@ -147,36 +185,62 @@ def tile_l1regressionmoeactionhead_pa_t_kernel(tc, x, W_qa, b_qa, W_qt, b_qt, ou
                     stop=True,
                 )
                 pp[(n, w)] = acc
+            q = qsb.tile([P, T], F32, name="q")
+            nc.scalar.activation(out=q[:], in_=pp[(n, 0)][:], func=ACT.Identity, bias=cstb[:, 0:1])
+            qq[n] = q
 
-        def biased(n):
-            for w in range(2):
-                q = qsb.tile([P, T], F32, name="q")
-                nc.scalar.activation(out=q[:], in_=pp[(n, w)][:], func=ACT.Identity, bias=cstb[:, w : w + 1])
-                qq[(n, w)] = q
-
-        def opose(n, w):
-            o = pso.tile([P, TI, D], F32, name="o", tag="o")
-            nc.tensor.matmul(o[:, 0, :], lhsT=qq[(n, w)][:, 0:P], rhs=ident[:], start=True, stop=True)
-            for i in range(1, TI):
-                nc.tensor.transpose(o[:, i, :], qq[(n, w)][:, P * i : P * i + P], ident[:])
-            oo[(n, w)] = o
-
-        def rope(n, w):
-            o = oo[(n, w)][:].rearrange("p i (h c e) -> p i h c e", h=2, e=2)
-            cos = tab[:, 0].rearrange("p i (c e) -> p i c e", e=2).unsqueeze(2).to_broadcast([P, TI, 2, J // 2, 2])
-            sin = tab[:, 1].rearrange("p i (c e) -> p i c e", e=2).unsqueeze(2).to_broadcast([P, TI, 2, J // 2, 2])
-            a = prod.tile([P, T], F32, name="prod_a")
-            b = prod.tile([P, T], F32, name="prod_b")
-            view = "p (i h c e) -> p i h c e"
-            nc.vector.tensor_tensor(out=a[:].rearrange(view, i=TI, h=2, e=2), in0=o, in1=cos, op=ALU.mult)
-            nc.vector.tensor_tensor(
-                out=b[:].rearrange(view, i=TI, h=2, e=2), in0=o[:, :, :, :, ::-1], in1=sin, op=ALU.mult
-            )
-            o_sb = ost.tile([P, TI * D], F32, name="o_sb")
-            nc.gpsimd.tensor_tensor(out=o_sb[:], in0=a[:], in1=b[:], op=ALU.add)
+        def store(n, w, o_sb):
             nc.sync.dma_start(out=outs[w][n, 0].rearrange("(p i) d -> p (i d)", i=TI), in_=o_sb[:])
 
-        xpose(0, second_on_vector=True)
+        def opose0(n):
+            o = pso.tile([P, TI, D], F32, name="o", tag="o")
+            for i in range(TI):
+                nc.tensor.transpose(o[:, i, :], qq[n][:, P * i : P * i + P], ident[:])
+            oo[n] = o
+            ab[(n, 0)] = []
+            for j in range(2):
+                t = prod.tile([P, T], F32, name="prod0%d" % j)
+                ab[(n, 0)].append(t)
+
+        def rope0(n, j):
+            o = oo[n][:].rearrange("p i (h c e) -> p i h c e", h=2, e=2)
+            view = "p (i h c e) -> p i h c e"
+            table = tab[:, j].rearrange("p i (c e) -> p i c e", e=2).unsqueeze(2).to_broadcast([P, TI, 2, J // 2, 2])
+            nc.vector.tensor_tensor(
+                out=ab[(n, 0)][j][:].rearrange(view, i=TI, h=2, e=2),
+                in0=o if j == 0 else o[:, :, :, :, ::-1],
+                in1=table,
+                op=ALU.mult,
+            )
+
+        def add0(n, engine):
+            o_sb = ost.tile([P, TI * D], F32, name="o_sb0")
+            engine.tensor_tensor(out=o_sb[:], in0=ab[(n, 0)][0][:], in1=ab[(n, 0)][1][:], op=ALU.add)
+            store(n, 0, o_sb)
+
+        def rope1(n):
+            ab[(n, 1)] = []
+            for j in range(2):
+                t = prod.tile([P, T], F32, name="prod1%d" % j)
+                nc.vector.scalar_tensor_tensor(
+                    out=t[:], in0=pp[(n, 1)][:], scalar=cstb[:, 1:2], in1=ftab[:, j, :], op0=ALU.add, op1=ALU.mult
+                )
+                ab[(n, 1)].append(t)
+
+        def opose1(n):
+            o = pss.tile([P, TI, D], F32, name="os", tag="os")
+            for i in range(TI):
+                for j, moving in ((0, ident), (1, perm)):
+                    nc.tensor.matmul(
+                        o[:, i, :], lhsT=ab[(n, 1)][j][:, P * i : P * i + P], rhs=moving[:],
+                        is_transpose=i > 0, start=j == 0, stop=j == 1,
+                    )
+            o_sb = ost.tile([P, TI * D], F32, name="o_sb1")
+            nc.scalar.copy(out=o_sb[:], in_=o[:].rearrange("p i d -> p (i d)"))
+            store(n, 1, o_sb)
+
+        xpose(0, 0, "scalar")
+        xpose(0, 1, "vector")
         wc = const.tile([P, 2 * D], U32, name="wc", align_bytes=64)
         ws = const.tile([P, 2 * D], U8, name="ws", align_bytes=64)
         nc.vector.quantize_mx(out=wc[:].bitcast(FP8X4), scales=ws[:], in_=wg[:])
@@ -185,22 +249,33 @@ def tile_l1regressionmoeactionhead_pa_t_kernel(tc, x, W_qa, b_qa, W_qt, b_qt, ou
         nc.tensor.transpose(setup_b[:], brow_f[:], ident[:])
         cstb = const.tile([P, 2], F32, name="cstb")
         nc.vector.tensor_copy(out=cstb[:], in_=setup_b[:, 0:2])
-        nc.scalar.activation(out=tab[:], in_=frac[:], func=ACT.Sin, scale=2.0 * math.pi)
-        xpose(1, second_on_vector=True)
+        nc.scalar.activation(out=ftab[:], in_=ffrac[:], func=ACT.Sin, scale=2.0 * math.pi)
+        xpose(1, 0, "scalar")
+        xpose(1, 1, "vector")
         mx(0)
-        biased(0)
         quant(1)
-        xpose(2)
+        nc.scalar.activation(out=tab[:], in_=frac[:], func=ACT.Sin, scale=2.0 * math.pi)
+        xpose(2, 0, "scalar")
+        xpose(2, 1, "scalar")
 
-        for k in range(NB):
-            opose(k, 0)
-            opose(k, 1)
-            if k + 1 < NB:
-                mx(k + 1)
-                biased(k + 1)
+        for k in range(NB + 1):
+            if k == 0:
+                opose0(0)
+                mx(1)
             if k + 3 < NB:
-                xpose(k + 3)
-            rope(k, 0)
-            if k + 2 < NB:
-                quant(k + 2)
-            rope(k, 1)
+                xpose(k + 3, 0, "scalar")
+            if k >= 1:
+                opose1(k - 1)
+            if k + 3 < NB:
+                xpose(k + 3, 1, "scalar")
+            if 1 <= k < NB:
+                opose0(k)
+            if 2 <= k + 1 < NB:
+                mx(k + 1)
+            if k < NB:
+                rope1(k)
+                rope0(k, 0)
+                if k + 2 < NB:
+                    quant(k + 2)
+                rope0(k, 1)
+                add0(k, nc.gpsimd if k + 1 < NB else nc.vector)

@@ -45,7 +45,7 @@ def tile_l1regressionmoeactionhead_pa_t_kernel(tc, x, W_qa, b_qa, W_qt, b_qt, ou
         w_sb = []
         for w, W in enumerate((W_qa, W_qt)):
             wt = const.tile([P, K], BF16, name="w_sb%d" % w)
-            nc.scalar.dma_start(out=wt[:], in_=W)
+            nc.sync.dma_start(out=wt[:], in_=W)
             w_sb.append(wt)
         brow = const.tile([P, D], BF16, name="brow")
         nc.gpsimd.memset(brow[:], 0.0)
@@ -54,13 +54,19 @@ def tile_l1regressionmoeactionhead_pa_t_kernel(tc, x, W_qa, b_qa, W_qt, b_qt, ou
         x_sb = []
         for n in range(NB):
             xt_in = xin.tile([P, TI * K], BF16, name="x_sb")
-            nc.sync.dma_start(out=xt_in[:], in_=x[n].rearrange("(p i) k -> p (i k)", i=TI))
+            rows = x[n].rearrange("(p i) k -> p (i k)", i=TI)
+            pieces = 2 if n == 0 else 1
+            wide = TI * K // pieces
+            for c in range(pieces):
+                nc.sync.dma_start(out=xt_in[:, wide * c : wide * c + wide], in_=rows[:, wide * c : wide * c + wide])
             x_sb.append(xt_in)
 
-        tok = const.tile([P, TI], I32, name="tok")
-        nc.gpsimd.iota(tok[:], pattern=[[1, TI]], base=0, channel_multiplier=TI)
-        tp = const.tile([P, P], I32, name="tp")
-        nc.gpsimd.iota(tp[:], pattern=[[TI, P]], base=0, channel_multiplier=0)
+        tok_col = const.tile([P, TI], F32, name="tok_col")
+        nc.gpsimd.iota(tok_col[:], pattern=[[1, TI]], base=0, channel_multiplier=TI, allow_small_or_imprecise_dtypes=True)
+        tok_row = const.tile([P, TI, P], F32, name="tok_row")
+        nc.gpsimd.iota(
+            tok_row[:], pattern=[[1, TI], [TI, P]], base=0, channel_multiplier=0, allow_small_or_imprecise_dtypes=True
+        )
         ident = const.tile([P, P], F32, name="ident")
         make_identity(nc, ident[:])
         perm = const.tile([P, P], F32, name="perm")
@@ -68,67 +74,64 @@ def tile_l1regressionmoeactionhead_pa_t_kernel(tc, x, W_qa, b_qa, W_qt, b_qt, ou
         perm_v = perm[:].rearrange("p (i e) -> p i e", e=2)
         nc.gpsimd.tensor_copy(out=perm_v[:, :, 0], in_=ident_v[:, :, 1])
         nc.gpsimd.tensor_copy(out=perm_v[:, :, 1], in_=ident_v[:, :, 0])
+
+        ratio = 10000.0 ** (-1.0 / J)
+        f2 = const.tile([P, 2, D], F32, name="f2")
+        nc.vector.memset(f2[:, 0, 0:1], 1.0)
+        nc.vector.tensor_scalar_mul(out=f2[:, 0, 0:1], in0=f2[:, 0, 0:1], scalar1=1.0 / (2.0 * math.pi))
+        junk = const.tile([P, 1], F32, name="junk")
+        nc.scalar.activation(out=junk[:], in_=f2[:, 0, 0:1], func=ACT.Sin)
+        for step in range(7):
+            width = 2**step
+            nc.vector.tensor_scalar_mul(
+                out=f2[:, 0, width : 2 * width], in0=f2[:, 0, 0:width],
+                scalar1=(ratio**width if width < J else 1.0),
+            )
+        own = f2[:, 0, :].rearrange("p (c e) -> p c e", e=2)
+        into = f2[:, 1, :].rearrange("p (c e) -> p c e", e=2)
+        nc.vector.tensor_copy(out=into[:, :, 0], in_=own[:, :, 1])
+        nc.vector.tensor_scalar_mul(out=into[:, :, 1], in0=own[:, :, 0], scalar1=-1.0)
+        freq = const.tile([P, 2, J], F32, name="freq")
+        pair = freq[:, 1, :].rearrange("p (c e) -> p c e", e=2)
+        half = f2[:, 0, 0:J].rearrange("p (c e) -> p c e", e=2)
+        nc.gpsimd.tensor_copy(out=freq[:, 0, :], in_=f2[:, 0, 0:J])
+        nc.gpsimd.tensor_scalar(out=pair[:, :, 0], in0=half[:, :, 0], scalar1=-1.0, scalar2=0.0, op0=ALU.mult, op1=ALU.add)
+        nc.gpsimd.tensor_copy(out=pair[:, :, 1], in_=half[:, :, 1])
         brow_f = const.tile([P, D], F32, name="brow_f")
         nc.gpsimd.tensor_copy(out=brow_f[:], in_=brow[:])
 
-        ratio = 10000.0 ** (-1.0 / J)
-        freq = const.tile([P, 2, J], F32, name="freq")
-        nc.vector.memset(freq[:, 0, 0:1], 1.0)
-        nc.vector.tensor_scalar_mul(out=freq[:, 0, 0:1], in0=freq[:, 0, 0:1], scalar1=1.0 / (2.0 * math.pi))
-        junk = const.tile([P, 1], F32, name="junk")
-        nc.scalar.activation(out=junk[:], in_=freq[:, 0, 0:1], func=ACT.Sin)
-        for step in range(6):
-            width = 2**step
-            nc.vector.tensor_scalar_mul(
-                out=freq[:, 0, width : 2 * width], in0=freq[:, 0, 0:width], scalar1=ratio**width
-            )
-        pair = freq[:].rearrange("p s (c e) -> p s c e", e=2)
-        nc.vector.tensor_scalar_mul(out=pair[:, 1, :, 0], in0=pair[:, 0, :, 0], scalar1=-1.0)
-        nc.vector.tensor_copy(out=pair[:, 1, :, 1], in_=pair[:, 0, :, 1])
-        tok_f = const.tile([P, TI], F32, name="tok_f")
-        nc.vector.tensor_copy(out=tok_f[:], in_=tok[:])
-
-        turns = const.tile([P, 2, TI, J], F32, name="turns")
-        whole = const.tile([P, 2, TI, J], I32, name="whole")
-        frac = const.tile([P, 2, TI, J], F32, name="frac")
-        tab = const.tile([P, 2, TI, J], F32, name="tab")
-        for i in range(TI):
-            nc.vector.tensor_scalar_mul(out=turns[:, :, i, :], in0=freq[:], scalar1=tok_f[:, i : i + 1])
-        nc.vector.tensor_scalar_add(out=whole[:, 0], in0=turns[:, 0], scalar1=0.25)
-        nc.vector.tensor_copy(out=whole[:, 1], in_=turns[:, 1])
-        nc.vector.scalar_tensor_tensor(
-            out=frac[:, 0], in0=turns[:, 0], scalar=0.25, in1=whole[:, 0], op0=ALU.add, op1=ALU.subtract
-        )
-        nc.vector.tensor_tensor(out=frac[:, 1], in0=turns[:, 1], in1=whole[:, 1], op=ALU.subtract)
-
-        f2 = const.tile([P, 2, 2, J], F32, name="f2")
-        for h in range(2):
-            nc.vector.tensor_copy(out=f2[:, 0, h, :], in_=freq[:, 0, :])
-            fs_v = f2[:, 1, h, :].rearrange("p (c e) -> p c e", e=2)
-            nc.vector.tensor_copy(out=fs_v[:, :, 0], in_=pair[:, 0, :, 1])
-            nc.vector.tensor_scalar_mul(out=fs_v[:, :, 1], in0=pair[:, 0, :, 0], scalar1=-1.0)
         setup_f = pso.tile([P, 2, P], F32, name="setup_f", tag="o")
         for c in range(2):
-            nc.tensor.transpose(setup_f[:, c, :], f2[:, c].rearrange("p h j -> p (h j)"), ident[:])
+            nc.tensor.transpose(setup_f[:, c, :], f2[:, c, :], ident[:])
         cstf = const.tile([P, 2], F32, name="cstf")
         nc.vector.tensor_copy(out=cstf[:], in_=setup_f[:, :, 0])
-        tf = const.tile([P, T], F32, name="tf")
-        for i in range(TI):
-            nc.vector.tensor_scalar_add(out=tf[:, P * i : P * i + P], in0=tp[:], scalar1=float(i))
-        fturns = const.tile([P, T], F32, name="fturns")
-        fwhole = const.tile([P, 2, T], I32, name="fwhole")
-        ffrac = const.tile([P, 2, T], F32, name="ffrac")
-        ftab = const.tile([P, 2, T], F32, name="ftab")
-        nc.vector.tensor_scalar(
-            out=fturns[:], in0=tf[:], scalar1=cstf[:, 0:1], scalar2=0.25, op0=ALU.mult, op1=ALU.add
-        )
-        nc.vector.tensor_scalar_mul(out=fwhole[:, 1, :], in0=tf[:], scalar1=cstf[:, 1:2])
-        nc.vector.tensor_copy(out=fwhole[:, 0, :], in_=fturns[:])
-        nc.vector.scalar_tensor_tensor(
-            out=ffrac[:, 1, :], in0=tf[:], scalar=cstf[:, 1:2], in1=fwhole[:, 1, :],
-            op0=ALU.mult, op1=ALU.subtract,
-        )
-        nc.vector.tensor_tensor(out=ffrac[:, 0, :], in0=fturns[:], in1=fwhole[:, 0, :], op=ALU.subtract)
+
+        shapes = {"f": [P, 2, T], "t": [P, 2, TI * J]}
+        turns, whole, frac, tab = {}, {}, {}, {}
+        for key in ("f", "t"):
+            turns[key] = const.tile(shapes[key], F32, name="turns_" + key)
+            whole[key] = const.tile(shapes[key], I32, name="whole_" + key)
+            frac[key] = const.tile(shapes[key], F32, name="frac_" + key)
+            tab[key] = const.tile(shapes[key], F32, name="tab_" + key)
+
+        def reduced(key):
+            t, w, f = turns[key], whole[key], frac[key]
+            nc.vector.tensor_scalar_add(out=w[:, 0, :], in0=t[:, 0, :], scalar1=0.25)
+            nc.vector.tensor_copy(out=w[:, 1, :], in_=t[:, 1, :])
+            nc.vector.scalar_tensor_tensor(
+                out=f[:, 0, :], in0=t[:, 0, :], scalar=0.25, in1=w[:, 0, :], op0=ALU.add, op1=ALU.subtract
+            )
+            nc.vector.tensor_tensor(out=f[:, 1, :], in0=t[:, 1, :], in1=w[:, 1, :], op=ALU.subtract)
+
+        def sines(key):
+            nc.scalar.activation(out=tab[key][:], in_=frac[key][:], func=ACT.Sin, scale=2.0 * math.pi)
+
+        for c in range(2):
+            nc.scalar.activation(
+                out=turns["f"][:, c, :], in_=tok_row[:].rearrange("p i t -> p (i t)"), func=ACT.Identity,
+                scale=cstf[:, c : c + 1],
+            )
+        reduced("f")
 
         wt_ps = psx.tile([P, 4, P], F32, name="wt_ps", tag="xt")
         for w in range(2):
@@ -140,6 +143,11 @@ def tile_l1regressionmoeactionhead_pa_t_kernel(tc, x, W_qa, b_qa, W_qt, b_qt, ou
             out=wg[:].bitcast(F32).rearrange("p (w d u) -> p w d u", w=2, u=2),
             in_=wt_ps[:].rearrange("p (w u) d -> p w d u", u=2),
         )
+        turns_t = turns["t"][:].rearrange("p c (i j) -> p c i j", i=TI)
+        for i in range(TI):
+            nc.scalar.activation(
+                out=turns_t[:, :, i, :], in_=freq[:], func=ACT.Identity, scale=tok_col[:, i : i + 1]
+            )
 
         xg = {}
         xq = {}
@@ -196,16 +204,17 @@ def tile_l1regressionmoeactionhead_pa_t_kernel(tc, x, W_qa, b_qa, W_qt, b_qt, ou
             o = pso.tile([P, TI, D], F32, name="o", tag="o")
             for i in range(TI):
                 nc.tensor.transpose(o[:, i, :], qq[n][:, P * i : P * i + P], ident[:])
-            oo[n] = o
+            oo[(n, 0)] = o
             ab[(n, 0)] = []
             for j in range(2):
                 t = prod.tile([P, T], F32, name="prod0%d" % j)
                 ab[(n, 0)].append(t)
 
         def rope0(n, j):
-            o = oo[n][:].rearrange("p i (h c e) -> p i h c e", h=2, e=2)
+            o = oo[(n, 0)][:].rearrange("p i (h c e) -> p i h c e", h=2, e=2)
             view = "p (i h c e) -> p i h c e"
-            table = tab[:, j].rearrange("p i (c e) -> p i c e", e=2).unsqueeze(2).to_broadcast([P, TI, 2, J // 2, 2])
+            table = tab["t"][:, j, :].rearrange("p (i c e) -> p i c e", i=TI, e=2)
+            table = table.unsqueeze(2).to_broadcast([P, TI, 2, J // 2, 2])
             nc.vector.tensor_tensor(
                 out=ab[(n, 0)][j][:].rearrange(view, i=TI, h=2, e=2),
                 in0=o if j == 0 else o[:, :, :, :, ::-1],
@@ -223,7 +232,7 @@ def tile_l1regressionmoeactionhead_pa_t_kernel(tc, x, W_qa, b_qa, W_qt, b_qt, ou
             for j in range(2):
                 t = prod.tile([P, T], F32, name="prod1%d" % j)
                 nc.vector.scalar_tensor_tensor(
-                    out=t[:], in0=pp[(n, 1)][:], scalar=cstb[:, 1:2], in1=ftab[:, j, :], op0=ALU.add, op1=ALU.mult
+                    out=t[:], in0=pp[(n, 1)][:], scalar=cstb[:, 1:2], in1=tab["f"][:, j, :], op0=ALU.add, op1=ALU.mult
                 )
                 ab[(n, 1)].append(t)
 
@@ -233,34 +242,37 @@ def tile_l1regressionmoeactionhead_pa_t_kernel(tc, x, W_qa, b_qa, W_qt, b_qt, ou
                 for j, moving in ((0, ident), (1, perm)):
                     nc.tensor.matmul(
                         o[:, i, :], lhsT=ab[(n, 1)][j][:, P * i : P * i + P], rhs=moving[:],
-                        is_transpose=i > 0, start=j == 0, stop=j == 1,
+                        is_transpose=True, start=j == 0, stop=j == 1,
                     )
             o_sb = ost.tile([P, TI * D], F32, name="o_sb1")
             nc.scalar.copy(out=o_sb[:], in_=o[:].rearrange("p i d -> p (i d)"))
             store(n, 1, o_sb)
 
         xpose(0, 0, "scalar")
-        xpose(0, 1, "vector")
+        xpose(0, 1, "scalar")
+        sines("f")
         wc = const.tile([P, 2 * D], U32, name="wc", align_bytes=64)
         ws = const.tile([P, 2 * D], U8, name="ws", align_bytes=64)
         nc.vector.quantize_mx(out=wc[:].bitcast(FP8X4), scales=ws[:], in_=wg[:])
         quant(0)
+        reduced("t")
+        xpose(1, 0, "scalar")
+        xpose(1, 1, "scalar")
         setup_b = pso.tile([P, P], F32, name="setup_b", tag="o")
         nc.tensor.transpose(setup_b[:], brow_f[:], ident[:])
         cstb = const.tile([P, 2], F32, name="cstb")
         nc.vector.tensor_copy(out=cstb[:], in_=setup_b[:, 0:2])
-        nc.scalar.activation(out=ftab[:], in_=ffrac[:], func=ACT.Sin, scale=2.0 * math.pi)
-        xpose(1, 0, "scalar")
-        xpose(1, 1, "vector")
         mx(0)
+        sines("t")
+        rope1(0)
         quant(1)
-        nc.scalar.activation(out=tab[:], in_=frac[:], func=ACT.Sin, scale=2.0 * math.pi)
         xpose(2, 0, "scalar")
         xpose(2, 1, "scalar")
 
         for k in range(NB + 1):
+            if k <= 1:
+                opose0(k)
             if k == 0:
-                opose0(0)
                 mx(1)
             if k + 3 < NB:
                 xpose(k + 3, 0, "scalar")
@@ -268,12 +280,13 @@ def tile_l1regressionmoeactionhead_pa_t_kernel(tc, x, W_qa, b_qa, W_qt, b_qt, ou
                 opose1(k - 1)
             if k + 3 < NB:
                 xpose(k + 3, 1, "scalar")
-            if 1 <= k < NB:
+            if 2 <= k < NB:
                 opose0(k)
             if 2 <= k + 1 < NB:
                 mx(k + 1)
             if k < NB:
-                rope1(k)
+                if k >= 1:
+                    rope1(k)
                 rope0(k, 0)
                 if k + 2 < NB:
                     quant(k + 2)

@@ -19,6 +19,7 @@ T = 512
 K = 512
 D = 128
 J = 64
+TS = 2
 TI = 4
 
 FLOPS = 2 * NB * T * K * 2 * D
@@ -38,7 +39,8 @@ def tile_l1regressionmoeactionhead_pa_t_kernel(tc, x, W_qa, b_qa, W_qt, b_qt, ou
         psx = ctx.enter_context(tc.psum_pool(name="psx", bufs=2))
         ps0 = ctx.enter_context(tc.psum_pool(name="ps0", bufs=1))
         ps1 = ctx.enter_context(tc.psum_pool(name="ps1", bufs=2))
-        pso = ctx.enter_context(tc.psum_pool(name="pso", bufs=2))
+        pso = ctx.enter_context(tc.psum_pool(name="pso", bufs=1))
+        psq = ctx.enter_context(tc.psum_pool(name="psq", bufs=1))
         pss = ctx.enter_context(tc.psum_pool(name="pss", bufs=1))
         ctx.enter_context(tc.manual_schedule())
 
@@ -63,9 +65,9 @@ def tile_l1regressionmoeactionhead_pa_t_kernel(tc, x, W_qa, b_qa, W_qt, b_qt, ou
 
         tok_col = const.tile([P, TI], F32, name="tok_col")
         nc.gpsimd.iota(tok_col[:], pattern=[[1, TI]], base=0, channel_multiplier=TI, allow_small_or_imprecise_dtypes=True)
-        tok_row = const.tile([P, TI, P], F32, name="tok_row")
+        tok_row = const.tile([P, TS, P], F32, name="tok_row")
         nc.gpsimd.iota(
-            tok_row[:], pattern=[[1, TI], [TI, P]], base=0, channel_multiplier=0, allow_small_or_imprecise_dtypes=True
+            tok_row[:], pattern=[[1, TS], [TI, P]], base=0, channel_multiplier=0, allow_small_or_imprecise_dtypes=True
         )
         ident = const.tile([P, P], F32, name="ident")
         make_identity(nc, ident[:])
@@ -100,13 +102,13 @@ def tile_l1regressionmoeactionhead_pa_t_kernel(tc, x, W_qa, b_qa, W_qt, b_qt, ou
         brow_f = const.tile([P, D], F32, name="brow_f")
         nc.gpsimd.tensor_copy(out=brow_f[:], in_=brow[:])
 
-        setup_f = pso.tile([P, 2, P], F32, name="setup_f", tag="o")
+        setup_f = pso.tile([P, 2, P], F32, name="setup_f", tag="o0")
         for c in range(2):
             nc.tensor.transpose(setup_f[:, c, :], f2[:, c, :], ident[:])
         cstf = const.tile([P, 2], F32, name="cstf")
         nc.vector.tensor_copy(out=cstf[:], in_=setup_f[:, :, 0])
 
-        shapes = {"f": [P, 2, T], "t": [P, 2, TI * J]}
+        shapes = {"f": [P, 2, TS * P], "t": [P, 2, TI * J]}
         turns, whole, frac, tab = {}, {}, {}, {}
         for key in ("f", "t"):
             turns[key] = const.tile(shapes[key], F32, name="turns_" + key)
@@ -155,6 +157,7 @@ def tile_l1regressionmoeactionhead_pa_t_kernel(tc, x, W_qa, b_qa, W_qt, b_qt, ou
         qq = {}
         oo = {}
         ab = {}
+        osb = {}
 
         def xpose(n, h, engine):
             if h == 0:
@@ -193,60 +196,68 @@ def tile_l1regressionmoeactionhead_pa_t_kernel(tc, x, W_qa, b_qa, W_qt, b_qt, ou
                     stop=True,
                 )
                 pp[(n, w)] = acc
-            q = qsb.tile([P, T], F32, name="q")
-            nc.scalar.activation(out=q[:], in_=pp[(n, 0)][:], func=ACT.Identity, bias=cstb[:, 0:1])
-            qq[n] = q
-
-        def store(n, w, o_sb):
-            nc.sync.dma_start(out=outs[w][n, 0].rearrange("(p i) d -> p (i d)", i=TI), in_=o_sb[:])
-
-        def opose0(n):
-            o = pso.tile([P, TI, D], F32, name="o", tag="o")
-            for i in range(TI):
-                nc.tensor.transpose(o[:, i, :], qq[n][:, P * i : P * i + P], ident[:])
-            oo[(n, 0)] = o
-            ab[(n, 0)] = []
-            for j in range(2):
-                t = prod.tile([P, T], F32, name="prod0%d" % j)
-                ab[(n, 0)].append(t)
-
-        def rope0(n, j):
-            o = oo[(n, 0)][:].rearrange("p i (h c e) -> p i h c e", h=2, e=2)
-            view = "p (i h c e) -> p i h c e"
-            table = tab["t"][:, j, :].rearrange("p (i c e) -> p i c e", i=TI, e=2)
-            table = table.unsqueeze(2).to_broadcast([P, TI, 2, J // 2, 2])
-            nc.vector.tensor_tensor(
-                out=ab[(n, 0)][j][:].rearrange(view, i=TI, h=2, e=2),
-                in0=o if j == 0 else o[:, :, :, :, ::-1],
-                in1=table,
-                op=ALU.mult,
-            )
-
-        def add0(n, engine):
-            o_sb = ost.tile([P, TI * D], F32, name="o_sb0")
-            engine.tensor_tensor(out=o_sb[:], in0=ab[(n, 0)][0][:], in1=ab[(n, 0)][1][:], op=ALU.add)
-            store(n, 0, o_sb)
-
-        def rope1(n):
-            ab[(n, 1)] = []
-            for j in range(2):
-                t = prod.tile([P, T], F32, name="prod1%d" % j)
-                nc.vector.scalar_tensor_tensor(
-                    out=t[:], in0=pp[(n, 1)][:], scalar=cstb[:, 1:2], in1=tab["f"][:, j, :], op0=ALU.add, op1=ALU.mult
+            for w, i0 in ((1, TS), (0, 0)):
+                q = qsb.tile([P, (TI - i0) * P], F32, name="q%d" % w)
+                nc.scalar.activation(
+                    out=q[:], in_=pp[(n, w)][:, P * i0 :], func=ACT.Identity, bias=cstb[:, w : w + 1]
                 )
-                ab[(n, 1)].append(t)
+                qq[(n, w)] = q
 
-        def opose1(n):
-            o = pss.tile([P, TI, D], F32, name="os", tag="os")
-            for i in range(TI):
+        def store(n, w):
+            nc.sync.dma_start(out=outs[w][n, 0].rearrange("(p i) d -> p (i d)", i=TI), in_=osb[(n, w)][:])
+
+        def opose(n, w):
+            ni = TI - TS * w
+            o = (pso, psq)[w].tile([P, ni, D], F32, name="o%d" % w)
+            for i in range(ni):
+                nc.tensor.matmul(
+                    o[:, i, :], lhsT=qq[(n, w)][:, P * i : P * i + P], rhs=ident[:],
+                    is_transpose=w == 1 or i > 0, start=True, stop=True,
+                )
+            oo[(n, w)] = o
+
+        def rope(n, w):
+            ni = TI - TS * w
+            o = oo[(n, w)][:].rearrange("p i (h c e) -> p i h c e", h=2, e=2)
+            ab[(n, w)] = []
+            for j in range(2):
+                t = prod.tile([P, ni * D], F32, name="prod%d%d" % (w, j))
+                table = tab["t"][:, j, (TI - ni) * J :].rearrange("p (i c e) -> p i c e", i=ni, e=2)
+                nc.vector.tensor_tensor(
+                    out=t[:].rearrange("p (i h c e) -> p i h c e", i=ni, h=2, e=2),
+                    in0=o if j == 0 else o[:, :, :, :, ::-1],
+                    in1=table.unsqueeze(2).to_broadcast([P, ni, 2, J // 2, 2]),
+                    op=ALU.mult,
+                )
+                ab[(n, w)].append(t)
+
+        def add(n, w, engine):
+            if w == 0:
+                osb[(n, 0)] = ost.tile([P, TI * D], F32, name="o_sb0")
+            a, b = ab[(n, w)]
+            engine.tensor_tensor(out=osb[(n, w)][:, TS * w * D :], in0=a[:], in1=b[:], op=ALU.add)
+            store(n, w)
+
+        def rope_s(n):
+            ab[(n, "s")] = []
+            for j in range(2):
+                t = prod.tile([P, TS * P], F32, name="prods%d" % j)
+                nc.vector.scalar_tensor_tensor(
+                    out=t[:], in0=pp[(n, 1)][:, 0 : TS * P], scalar=cstb[:, 1:2], in1=tab["f"][:, j, :],
+                    op0=ALU.add, op1=ALU.mult,
+                )
+                ab[(n, "s")].append(t)
+
+        def opose_s(n):
+            o = pss.tile([P, TS, D], F32, name="os")
+            for i in range(TS):
                 for j, moving in ((0, ident), (1, perm)):
                     nc.tensor.matmul(
-                        o[:, i, :], lhsT=ab[(n, 1)][j][:, P * i : P * i + P], rhs=moving[:],
+                        o[:, i, :], lhsT=ab[(n, "s")][j][:, P * i : P * i + P], rhs=moving[:],
                         is_transpose=True, start=j == 0, stop=j == 1,
                     )
-            o_sb = ost.tile([P, TI * D], F32, name="o_sb1")
-            nc.scalar.copy(out=o_sb[:], in_=o[:].rearrange("p i d -> p (i d)"))
-            store(n, 1, o_sb)
+            osb[(n, 1)] = ost.tile([P, TI * D], F32, name="o_sb1")
+            nc.scalar.copy(out=osb[(n, 1)][:, 0 : TS * D], in_=o[:].rearrange("p i d -> p (i d)"))
 
         xpose(0, 0, "scalar")
         xpose(0, 1, "scalar")
@@ -258,37 +269,36 @@ def tile_l1regressionmoeactionhead_pa_t_kernel(tc, x, W_qa, b_qa, W_qt, b_qt, ou
         reduced("t")
         xpose(1, 0, "scalar")
         xpose(1, 1, "scalar")
-        setup_b = pso.tile([P, P], F32, name="setup_b", tag="o")
+        setup_b = psq.tile([P, P], F32, name="setup_b", tag="o1")
         nc.tensor.transpose(setup_b[:], brow_f[:], ident[:])
         cstb = const.tile([P, 2], F32, name="cstb")
         nc.vector.tensor_copy(out=cstb[:], in_=setup_b[:, 0:2])
         mx(0)
         sines("t")
-        rope1(0)
-        quant(1)
         xpose(2, 0, "scalar")
+        opose(0, 1)
+        opose(0, 0)
         xpose(2, 1, "scalar")
+        rope_s(0)
+        quant(1)
 
-        for k in range(NB + 1):
-            if k <= 1:
-                opose0(k)
-            if k == 0:
-                mx(1)
+        for k in range(NB):
+            if k >= 1:
+                rope_s(k)
+            if k + 1 < NB:
+                mx(k + 1)
             if k + 3 < NB:
                 xpose(k + 3, 0, "scalar")
-            if k >= 1:
-                opose1(k - 1)
+            opose_s(k)
             if k + 3 < NB:
                 xpose(k + 3, 1, "scalar")
-            if 2 <= k < NB:
-                opose0(k)
-            if 2 <= k + 1 < NB:
-                mx(k + 1)
-            if k < NB:
-                if k >= 1:
-                    rope1(k)
-                rope0(k, 0)
-                if k + 2 < NB:
-                    quant(k + 2)
-                rope0(k, 1)
-                add0(k, nc.gpsimd if k + 1 < NB else nc.vector)
+            rope(k, 1)
+            add(k, 1, nc.gpsimd)
+            if k + 1 < NB:
+                opose(k + 1, 1)
+            rope(k, 0)
+            if k + 2 < NB:
+                quant(k + 2)
+            add(k, 0, nc.gpsimd if k + 1 < NB else nc.vector)
+            if k + 1 < NB:
+                opose(k + 1, 0)

@@ -129,13 +129,18 @@ def tile_l1regressionmoeactionhead_pa_t_kernel(tc, x, W_qa, b_qa, W_qt, b_qt, ou
             nc.scalar.activation(out=tab[key][:], in_=frac[key][:], func=ACT.Sin, scale=2.0 * math.pi)
 
         for c in range(2):
-            nc.scalar.activation(
-                out=turns["f"][:, c, :], in_=tok_row[:].rearrange("p i t -> p (i t)"), func=ACT.Identity,
-                scale=cstf[:, c : c + 1],
+            nc.vector.tensor_scalar_mul(
+                out=turns["f"][:, c, :], in0=tok_row[:].rearrange("p i t -> p (i t)"), scalar1=cstf[:, c : c + 1]
             )
+        turns_t = turns["t"][:].rearrange("p c (i j) -> p c i j", i=TI)
+        for i in range(TI):
+            nc.scalar.activation(
+                out=turns_t[:, :, i, :], in_=freq[:], func=ACT.Identity, scale=tok_col[:, i : i + 1]
+            )
+
         reduced("f")
 
-        wt_ps = psx.tile([P, 4, P], F32, name="wt_ps", tag="xt")
+        wt_ps = ps1.tile([P, 4, P], F32, name="wt_ps", tag="acc1")
         for w in range(2):
             ww = w_sb[w][:].bitcast(F32)
             for u in range(2):
@@ -145,12 +150,6 @@ def tile_l1regressionmoeactionhead_pa_t_kernel(tc, x, W_qa, b_qa, W_qt, b_qt, ou
             out=wg[:].bitcast(F32).rearrange("p (w d u) -> p w d u", w=2, u=2),
             in_=wt_ps[:].rearrange("p (w u) d -> p w d u", u=2),
         )
-        turns_t = turns["t"][:].rearrange("p c (i j) -> p c i j", i=TI)
-        for i in range(TI):
-            nc.scalar.activation(
-                out=turns_t[:, :, i, :], in_=freq[:], func=ACT.Identity, scale=tok_col[:, i : i + 1]
-            )
-
         xg = {}
         xq = {}
         pp = {}
@@ -196,6 +195,8 @@ def tile_l1regressionmoeactionhead_pa_t_kernel(tc, x, W_qa, b_qa, W_qt, b_qt, ou
                     stop=True,
                 )
                 pp[(n, w)] = acc
+
+        def biased(n):
             for w, i0 in ((1, TS), (0, 0)):
                 q = qsb.tile([P, (TI - i0) * P], F32, name="q%d" % w)
                 nc.scalar.activation(
@@ -208,17 +209,17 @@ def tile_l1regressionmoeactionhead_pa_t_kernel(tc, x, W_qa, b_qa, W_qt, b_qt, ou
 
         def opose(n, w):
             ni = TI - TS * w
-            o = (pso, psq)[w].tile([P, ni, D], F32, name="o%d" % w)
+            o = (pso, psq)[w].tile([P, TI, D], F32, name="o%d" % w)
             for i in range(ni):
                 nc.tensor.matmul(
                     o[:, i, :], lhsT=qq[(n, w)][:, P * i : P * i + P], rhs=ident[:],
-                    is_transpose=w == 1 or i > 0, start=True, stop=True,
+                    is_transpose=w == 0 or i > 0, start=True, stop=True,
                 )
             oo[(n, w)] = o
 
         def rope(n, w):
             ni = TI - TS * w
-            o = oo[(n, w)][:].rearrange("p i (h c e) -> p i h c e", h=2, e=2)
+            o = oo[(n, w)][:, 0:ni, :].rearrange("p i (h c e) -> p i h c e", h=2, e=2)
             ab[(n, w)] = []
             for j in range(2):
                 t = prod.tile([P, ni * D], F32, name="prod%d%d" % (w, j))
@@ -236,9 +237,9 @@ def tile_l1regressionmoeactionhead_pa_t_kernel(tc, x, W_qa, b_qa, W_qt, b_qt, ou
                 osb[(n, 0)] = ost.tile([P, TI * D], F32, name="o_sb0")
             a, b = ab[(n, w)]
             engine.tensor_tensor(out=osb[(n, w)][:, TS * w * D :], in0=a[:], in1=b[:], op=ALU.add)
-            store(n, w)
 
         def rope_s(n):
+            osb[(n, 1)] = ost.tile([P, TI * D], F32, name="o_sb1")
             ab[(n, "s")] = []
             for j in range(2):
                 t = prod.tile([P, TS * P], F32, name="prods%d" % j)
@@ -249,18 +250,17 @@ def tile_l1regressionmoeactionhead_pa_t_kernel(tc, x, W_qa, b_qa, W_qt, b_qt, ou
                 ab[(n, "s")].append(t)
 
         def opose_s(n):
-            o = pss.tile([P, TS, D], F32, name="os")
+            o = pss.tile([P, TI, D], F32, name="os")
             for i in range(TS):
                 for j, moving in ((0, ident), (1, perm)):
                     nc.tensor.matmul(
                         o[:, i, :], lhsT=ab[(n, "s")][j][:, P * i : P * i + P], rhs=moving[:],
                         is_transpose=True, start=j == 0, stop=j == 1,
                     )
-            osb[(n, 1)] = ost.tile([P, TI * D], F32, name="o_sb1")
-            nc.scalar.copy(out=osb[(n, 1)][:, 0 : TS * D], in_=o[:].rearrange("p i d -> p (i d)"))
+            nc.scalar.copy(out=osb[(n, 1)][:, 0 : TS * D], in_=o[:, 0:TS, :].rearrange("p i d -> p (i d)"))
 
         xpose(0, 0, "scalar")
-        xpose(0, 1, "scalar")
+        xpose(0, 1, "vector")
         sines("f")
         wc = const.tile([P, 2 * D], U32, name="wc", align_bytes=64)
         ws = const.tile([P, 2 * D], U8, name="ws", align_bytes=64)
@@ -274,6 +274,7 @@ def tile_l1regressionmoeactionhead_pa_t_kernel(tc, x, W_qa, b_qa, W_qt, b_qt, ou
         cstb = const.tile([P, 2], F32, name="cstb")
         nc.vector.tensor_copy(out=cstb[:], in_=setup_b[:, 0:2])
         mx(0)
+        biased(0)
         sines("t")
         xpose(2, 0, "scalar")
         opose(0, 1)
@@ -283,22 +284,25 @@ def tile_l1regressionmoeactionhead_pa_t_kernel(tc, x, W_qa, b_qa, W_qt, b_qt, ou
         quant(1)
 
         for k in range(NB):
-            if k >= 1:
-                rope_s(k)
-            if k + 1 < NB:
+            last = k + 1 == NB
+            if not last:
                 mx(k + 1)
+                biased(k + 1)
             if k + 3 < NB:
                 xpose(k + 3, 0, "scalar")
-            opose_s(k)
-            if k + 3 < NB:
                 xpose(k + 3, 1, "scalar")
+            if k >= 1:
+                rope_s(k)
             rope(k, 1)
             add(k, 1, nc.gpsimd)
-            if k + 1 < NB:
+            if not last:
                 opose(k + 1, 1)
             rope(k, 0)
             if k + 2 < NB:
                 quant(k + 2)
-            add(k, 0, nc.gpsimd if k + 1 < NB else nc.vector)
-            if k + 1 < NB:
+            add(k, 0, nc.vector if last else nc.gpsimd)
+            if not last:
                 opose(k + 1, 0)
+            opose_s(k)
+            store(k, 1)
+            store(k, 0)

@@ -83,32 +83,33 @@ def tile_l1regressionmoeactionhead_pa_t_kernel(tc, x, W_qa, b_qa, W_qt, b_qt, ou
         nc.vector.tensor_scalar_mul(out=f2[:, 0, 0:1], in0=f2[:, 0, 0:1], scalar1=1.0 / (2.0 * math.pi))
         junk = const.tile([P, 1], F32, name="junk")
         nc.scalar.activation(out=junk[:], in_=f2[:, 0, 0:1], func=ACT.Sin)
-        for step in range(7):
-            width = 2**step
-            nc.vector.tensor_scalar_mul(
-                out=f2[:, 0, width : 2 * width], in0=f2[:, 0, 0:width],
-                scalar1=(ratio**width if width < J else 1.0),
-            )
+        width = 1
+        while width < D:
+            for m in range(1, 4 if width < J else 2):
+                nc.vector.tensor_scalar_mul(
+                    out=f2[:, 0, width * m : width * (m + 1)], in0=f2[:, 0, 0:width],
+                    scalar1=(ratio ** (width * m) if width < J else 1.0),
+                )
+            width *= 4 if width < J else 2
         own = f2[:, 0, :].rearrange("p (c e) -> p c e", e=2)
         into = f2[:, 1, :].rearrange("p (c e) -> p c e", e=2)
         nc.vector.tensor_copy(out=into[:, :, 0], in_=own[:, :, 1])
         nc.vector.tensor_scalar_mul(out=into[:, :, 1], in0=own[:, :, 0], scalar1=-1.0)
-        freq = const.tile([P, 2, J], F32, name="freq")
-        pair = freq[:, 1, :].rearrange("p (c e) -> p c e", e=2)
-        half = f2[:, 0, 0:J].rearrange("p (c e) -> p c e", e=2)
-        nc.gpsimd.tensor_copy(out=freq[:, 0, :], in_=f2[:, 0, 0:J])
-        nc.gpsimd.tensor_scalar(out=pair[:, :, 0], in0=half[:, :, 0], scalar1=-1.0, scalar2=0.0, op0=ALU.mult, op1=ALU.add)
-        nc.gpsimd.tensor_copy(out=pair[:, :, 1], in_=half[:, :, 1])
         brow_f = const.tile([P, D], F32, name="brow_f")
         nc.gpsimd.tensor_copy(out=brow_f[:], in_=brow[:])
 
+        wt_ps = ps1.tile([P, 4, P], F32, name="wt_ps", tag="acc1")
+        for w in range(2):
+            ww = w_sb[w][:].bitcast(F32)
+            for u in range(2):
+                nc.tensor.transpose(wt_ps[:, 2 * w + u, :], ww[:, u : K // 2 : 2], ident[:])
         setup_f = pso.tile([P, 2, P], F32, name="setup_f", tag="o0")
         for c in range(2):
             nc.tensor.transpose(setup_f[:, c, :], f2[:, c, :], ident[:])
         cstf = const.tile([P, 2], F32, name="cstf")
         nc.vector.tensor_copy(out=cstf[:], in_=setup_f[:, :, 0])
 
-        shapes = {"f": [P, 2, TS * P], "t": [P, 2, TI * J]}
+        shapes = {"f": [P, 1, 2, TS * P], "t": [P, TI, 2, J]}
         turns, whole, frac, tab = {}, {}, {}, {}
         for key in ("f", "t"):
             turns[key] = const.tile(shapes[key], F32, name="turns_" + key)
@@ -118,33 +119,28 @@ def tile_l1regressionmoeactionhead_pa_t_kernel(tc, x, W_qa, b_qa, W_qt, b_qt, ou
 
         def reduced(key):
             t, w, f = turns[key], whole[key], frac[key]
-            nc.vector.tensor_scalar_add(out=w[:, 0, :], in0=t[:, 0, :], scalar1=0.25)
-            nc.vector.tensor_copy(out=w[:, 1, :], in_=t[:, 1, :])
+            cos, sin = (slice(None), slice(None), 0), (slice(None), slice(None), 1)
+            nc.vector.tensor_scalar_add(out=w[cos], in0=t[cos], scalar1=0.25)
+            nc.vector.tensor_copy(out=w[sin], in_=t[sin])
             nc.vector.scalar_tensor_tensor(
-                out=f[:, 0, :], in0=t[:, 0, :], scalar=0.25, in1=w[:, 0, :], op0=ALU.add, op1=ALU.subtract
+                out=f[cos], in0=t[cos], scalar=0.25, in1=w[cos], op0=ALU.add, op1=ALU.subtract
             )
-            nc.vector.tensor_tensor(out=f[:, 1, :], in0=t[:, 1, :], in1=w[:, 1, :], op=ALU.subtract)
+            nc.vector.tensor_tensor(out=f[sin], in0=t[sin], in1=w[sin], op=ALU.subtract)
 
         def sines(key):
             nc.scalar.activation(out=tab[key][:], in_=frac[key][:], func=ACT.Sin, scale=2.0 * math.pi)
 
         for c in range(2):
             nc.vector.tensor_scalar_mul(
-                out=turns["f"][:, c, :], in0=tok_row[:].rearrange("p i t -> p (i t)"), scalar1=cstf[:, c : c + 1]
+                out=turns["f"][:, 0, c, :], in0=tok_row[:].rearrange("p i t -> p (i t)"), scalar1=cstf[:, c : c + 1]
             )
-        turns_t = turns["t"][:].rearrange("p c (i j) -> p c i j", i=TI)
         for i in range(TI):
             nc.scalar.activation(
-                out=turns_t[:, :, i, :], in_=freq[:], func=ACT.Identity, scale=tok_col[:, i : i + 1]
+                out=turns["t"][:, i, :, :], in_=f2[:, :, 0:J], func=ACT.Identity, scale=tok_col[:, i : i + 1]
             )
 
         reduced("f")
 
-        wt_ps = ps1.tile([P, 4, P], F32, name="wt_ps", tag="acc1")
-        for w in range(2):
-            ww = w_sb[w][:].bitcast(F32)
-            for u in range(2):
-                nc.tensor.transpose(wt_ps[:, 2 * w + u, :], ww[:, u : K // 2 : 2], ident[:])
         wg = const.tile([P, 2 * D * 4], BF16, name="wg", align_bytes=64)
         nc.scalar.copy(
             out=wg[:].bitcast(F32).rearrange("p (w d u) -> p w d u", w=2, u=2),
@@ -219,42 +215,44 @@ def tile_l1regressionmoeactionhead_pa_t_kernel(tc, x, W_qa, b_qa, W_qt, b_qt, ou
 
         def rope(n, w):
             ni = TI - TS * w
-            o = oo[(n, w)][:, 0:ni, :].rearrange("p i (h c e) -> p i h c e", h=2, e=2)
-            ab[(n, w)] = []
-            for j in range(2):
-                t = prod.tile([P, ni * D], F32, name="prod%d%d" % (w, j))
-                table = tab["t"][:, j, (TI - ni) * J :].rearrange("p (i c e) -> p i c e", i=ni, e=2)
-                nc.vector.tensor_tensor(
-                    out=t[:].rearrange("p (i h c e) -> p i h c e", i=ni, h=2, e=2),
-                    in0=o if j == 0 else o[:, :, :, :, ::-1],
-                    in1=table.unsqueeze(2).to_broadcast([P, ni, 2, J // 2, 2]),
-                    op=ALU.mult,
-                )
-                ab[(n, w)].append(t)
+            o = oo[(n, w)][:, 0:ni, :].unsqueeze(2).to_broadcast([P, ni, 2, D])
+            table = tab["t"][:, TI - ni :, :, :].unsqueeze(3).to_broadcast([P, ni, 2, 2, J])
+            t = prod.tile([P, 2, ni * D], F32, name="prod%d" % w)
+            nc.vector.tensor_tensor(
+                out=t[:].rearrange("p c (i h j) -> p i c h j", i=ni, h=2),
+                in0=o.rearrange("p i c (h j) -> p i c h j", h=2),
+                in1=table,
+                op=ALU.mult,
+            )
+            ab[(n, w)] = t
 
         def add(n, w, engine):
             if w == 0:
                 osb[(n, 0)] = ost.tile([P, TI * D], F32, name="o_sb0")
-            a, b = ab[(n, w)]
-            engine.tensor_tensor(out=osb[(n, w)][:, TS * w * D :], in0=a[:], in1=b[:], op=ALU.add)
+            t = ab[(n, w)]
+            view = "p (f e) -> p f e"
+            engine.tensor_tensor(
+                out=osb[(n, w)][:, TS * w * D :].rearrange(view, e=2),
+                in0=t[:, 0, :].rearrange(view, e=2),
+                in1=t[:, 1, :].rearrange(view, e=2)[:, :, ::-1],
+                op=ALU.add,
+            )
 
         def rope_s(n):
             osb[(n, 1)] = ost.tile([P, TI * D], F32, name="o_sb1")
-            ab[(n, "s")] = []
-            for j in range(2):
-                t = prod.tile([P, TS * P], F32, name="prods%d" % j)
-                nc.vector.scalar_tensor_tensor(
-                    out=t[:], in0=pp[(n, 1)][:, 0 : TS * P], scalar=cstb[:, 1:2], in1=tab["f"][:, j, :],
-                    op0=ALU.add, op1=ALU.mult,
-                )
-                ab[(n, "s")].append(t)
+            t = prod.tile([P, 2, TS * P], F32, name="prods")
+            nc.vector.scalar_tensor_tensor(
+                out=t[:], in0=pp[(n, 1)][:, 0 : TS * P].unsqueeze(1).to_broadcast([P, 2, TS * P]),
+                scalar=cstb[:, 1:2], in1=tab["f"][:, 0], op0=ALU.add, op1=ALU.mult,
+            )
+            ab[(n, "s")] = t
 
         def opose_s(n):
             o = pss.tile([P, TI, D], F32, name="os")
             for i in range(TS):
                 for j, moving in ((0, ident), (1, perm)):
                     nc.tensor.matmul(
-                        o[:, i, :], lhsT=ab[(n, "s")][j][:, P * i : P * i + P], rhs=moving[:],
+                        o[:, i, :], lhsT=ab[(n, "s")][:, j, P * i : P * i + P], rhs=moving[:],
                         is_transpose=True, start=j == 0, stop=j == 1,
                     )
             nc.scalar.copy(out=osb[(n, 1)][:, 0 : TS * D], in_=o[:, 0:TS, :].rearrange("p i d -> p (i d)"))

import math
from contextlib import ExitStack

import concourse.mybir as mybir
from concourse.masks import make_identity

F32 = mybir.dt.float32
BF16 = mybir.dt.bfloat16
I32 = mybir.dt.int32
U32 = mybir.dt.uint32
U8 = mybir.dt.uint8
FP8X4 = mybir.dt.float8_e4m3fn_x4
ALU = mybir.AluOpType
ACT = mybir.ActivationFunctionType

P = 128
NB = 16
T = 512
K = 512
D = 128
J = 64
TS = 2
TI = 4

FLOPS = 2 * NB * T * K * 2 * D


def tile_l1regressionmoeactionhead_pa_t_kernel(tc, x, W_qa, b_qa, W_qt, b_qt, out_0, out_1):
    nc = tc.nc
    outs = (out_0, out_1)
    with ExitStack() as ctx:
        const = ctx.enter_context(tc.tile_pool(name="const", bufs=1))
        xin = ctx.enter_context(tc.tile_pool(name="xin", bufs=NB))
        grp = ctx.enter_context(tc.tile_pool(name="grp", bufs=3))
        cod = ctx.enter_context(tc.tile_pool(name="cod", bufs=3))
        qsb = ctx.enter_context(tc.tile_pool(name="qsb", bufs=2))
        prod = ctx.enter_context(tc.tile_pool(name="prod", bufs=3))
        ost = ctx.enter_context(tc.tile_pool(name="ost", bufs=6))
        psx = ctx.enter_context(tc.psum_pool(name="psx", bufs=2))
        ps0 = ctx.enter_context(tc.psum_pool(name="ps0", bufs=1))
        ps1 = ctx.enter_context(tc.psum_pool(name="ps1", bufs=2))
        pso = ctx.enter_context(tc.psum_pool(name="pso", bufs=1))
        psq = ctx.enter_context(tc.psum_pool(name="psq", bufs=1))
        pss = ctx.enter_context(tc.psum_pool(name="pss", bufs=1))
        ctx.enter_context(tc.manual_schedule())

        w_sb = []
        for w, W in enumerate((W_qa, W_qt)):
            wt = const.tile([P, K], BF16, name="w_sb%d" % w)
            nc.sync.dma_start(out=wt[:], in_=W)
            w_sb.append(wt)
        brow = const.tile([P, D], BF16, name="brow")
        nc.gpsimd.memset(brow[:], 0.0)
        nc.scalar.dma_start(out=brow[0:1, :], in_=b_qa.unsqueeze(0))
        nc.scalar.dma_start(out=brow[1:2, :], in_=b_qt.unsqueeze(0))
        x_sb = []
        for n in range(NB):
            xt_in = xin.tile([P, TI * K], BF16, name="x_sb")
            rows = x[n].rearrange("(p i) k -> p (i k)", i=TI)
            pieces = 2 if n == 0 else 1
            wide = TI * K // pieces
            for c in range(pieces):
                nc.sync.dma_start(out=xt_in[:, wide * c : wide * c + wide], in_=rows[:, wide * c : wide * c + wide])
            x_sb.append(xt_in)

        tok_col = const.tile([P, TI], F32, name="tok_col")
        nc.gpsimd.iota(tok_col[:], pattern=[[1, TI]], base=0, channel_multiplier=TI, allow_small_or_imprecise_dtypes=True)
        tok_row = const.tile([P, TS, P], F32, name="tok_row")
        nc.gpsimd.iota(
            tok_row[:], pattern=[[1, TS], [TI, P]], base=0, channel_multiplier=0, allow_small_or_imprecise_dtypes=True
        )
        ident = const.tile([P, P], F32, name="ident")
        make_identity(nc, ident[:])
        perm = const.tile([P, P], F32, name="perm")
        ident_v = ident[:].rearrange("p (i e) -> p i e", e=2)
        perm_v = perm[:].rearrange("p (i e) -> p i e", e=2)
        nc.gpsimd.tensor_copy(out=perm_v[:, :, 0], in_=ident_v[:, :, 1])
        nc.gpsimd.tensor_copy(out=perm_v[:, :, 1], in_=ident_v[:, :, 0])

        ratio = 10000.0 ** (-1.0 / J)
        f2 = const.tile([P, 2, D], F32, name="f2")
        nc.vector.memset(f2[:, 0, 0:1], 1.0)
        nc.vector.tensor_scalar_mul(out=f2[:, 0, 0:1], in0=f2[:, 0, 0:1], scalar1=1.0 / (2.0 * math.pi))
        junk = const.tile([P, 1], F32, name="junk")
        nc.scalar.activation(out=junk[:], in_=f2[:, 0, 0:1], func=ACT.Sin)
        width = 1
        while width < D:
            for m in range(1, 4 if width < J else 2):
                nc.vector.tensor_scalar_mul(
                    out=f2[:, 0, width * m : width * (m + 1)], in0=f2[:, 0, 0:width],
                    scalar1=(ratio ** (width * m) if width < J else 1.0),
                )
            width *= 4 if width < J else 2
        own = f2[:, 0, :].rearrange("p (c e) -> p c e", e=2)
        into = f2[:, 1, :].rearrange("p (c e) -> p c e", e=2)
        nc.vector.tensor_copy(out=into[:, :, 0], in_=own[:, :, 1])
        nc.vector.tensor_scalar_mul(out=into[:, :, 1], in0=own[:, :, 0], scalar1=-1.0)
        brow_f = const.tile([P, D], F32, name="brow_f")
        nc.gpsimd.tensor_copy(out=brow_f[:], in_=brow[:])

        wt_ps = ps1.tile([P, 4, P], F32, name="wt_ps", tag="acc1")
        for w in range(2):
            ww = w_sb[w][:].bitcast(F32)
            for u in range(2):
                nc.tensor.transpose(wt_ps[:, 2 * w + u, :], ww[:, u : K // 2 : 2], ident[:])
        setup_f = pso.tile([P, 2, P], F32, name="setup_f", tag="o0")
        for c in range(2):
            nc.tensor.transpose(setup_f[:, c, :], f2[:, c, :], ident[:])
        cstf = const.tile([P, 2], F32, name="cstf")
        nc.vector.tensor_copy(out=cstf[:], in_=setup_f[:, :, 0])

        shapes = {"f": [P, 1, 2, TS * P], "t": [P, TI, 2, J]}
        turns, whole, frac, tab = {}, {}, {}, {}
        for key in ("f", "t"):
            turns[key] = const.tile(shapes[key], F32, name="turns_" + key)
            whole[key] = const.tile(shapes[key], I32, name="whole_" + key)
            frac[key] = const.tile(shapes[key], F32, name="frac_" + key)
            tab[key] = const.tile(shapes[key], F32, name="tab_" + key)

        def reduced(key):
            t, w, f = turns[key], whole[key], frac[key]
            cos, sin = (slice(None), slice(None), 0), (slice(None), slice(None), 1)
            nc.vector.tensor_scalar_add(out=w[cos], in0=t[cos], scalar1=0.25)
            nc.vector.tensor_copy(out=w[sin], in_=t[sin])
            nc.vector.scalar_tensor_tensor(
                out=f[cos], in0=t[cos], scalar=0.25, in1=w[cos], op0=ALU.add, op1=ALU.subtract
            )
            nc.vector.tensor_tensor(out=f[sin], in0=t[sin], in1=w[sin], op=ALU.subtract)

        def sines(key):
            nc.scalar.activation(out=tab[key][:], in_=frac[key][:], func=ACT.Sin, scale=2.0 * math.pi)

        for c in range(2):
            nc.vector.tensor_scalar_mul(
                out=turns["f"][:, 0, c, :], in0=tok_row[:].rearrange("p i t -> p (i t)"), scalar1=cstf[:, c : c + 1]
            )
        for i in range(TI):
            nc.scalar.activation(
                out=turns["t"][:, i, :, :], in_=f2[:, :, 0:J], func=ACT.Identity, scale=tok_col[:, i : i + 1]
            )

        reduced("f")

        wg = const.tile([P, 2 * D * 4], BF16, name="wg", align_bytes=64)
        nc.scalar.copy(
            out=wg[:].bitcast(F32).rearrange("p (w d u) -> p w d u", w=2, u=2),
            in_=wt_ps[:].rearrange("p (w u) d -> p w d u", u=2),
        )
        xg = {}
        xq = {}
        pp = {}
        qq = {}
        oo = {}
        ab = {}
        osb = {}

        def xpose(n, h, engine):
            if h == 0:
                xg[n] = grp.tile([P, TI * K], BF16, name="xg", align_bytes=64)
            gw = xg[n][:].bitcast(F32)
            xw = x_sb[n][:].bitcast(F32)
            xt = psx.tile([P, 2, 2, P], F32, name="xt", tag="xt")
            for i2 in range(2):
                for u in range(2):
                    c0 = (2 * h + i2) * 256
                    nc.tensor.transpose(xt[:, i2, u, :], xw[:, c0 + u : c0 + 256 : 2], ident[:])
            dst = gw[:, 512 * h : 512 * h + 512].rearrange("p (i t u) -> p i t u", i=2, u=2)
            src = xt[:].rearrange("p i u t -> p i t u")
            if engine == "vector":
                nc.vector.tensor_copy(out=dst, in_=src)
            else:
                nc.scalar.copy(out=dst, in_=src)

        def quant(n):
            c = cod.tile([P, T], U32, name="xc", align_bytes=64)
            s = cod.tile([P, T], U8, name="xs", align_bytes=64)
            nc.vector.quantize_mx(out=c[:].bitcast(FP8X4), scales=s[:], in_=xg[n][:])
            xq[n] = (c, s)

        def mx(n):
            c, s = xq[n]
            for w, pool in ((1, ps1), (0, ps0)):
                acc = pool.tile([P, T], F32, name="acc%d" % w)
                nc.tensor.matmul_mx(
                    out=acc[:],
                    lhsT=wc[:, D * w : D * w + D].bitcast(FP8X4),
                    lhsT_scale=ws[:, D * w : D * w + D],
                    rhs=c[:].bitcast(FP8X4),
                    rhs_scale=s[:],
                    start=True,
                    stop=True,
                )
                pp[(n, w)] = acc

        def biased(n):
            for w, i0 in ((1, TS), (0, 0)):
                q = qsb.tile([P, (TI - i0) * P], F32, name="q%d" % w)
                nc.scalar.activation(
                    out=q[:], in_=pp[(n, w)][:, P * i0 :], func=ACT.Identity, bias=cstb[:, w : w + 1]
                )
                qq[(n, w)] = q

        def store(n, w):
            nc.sync.dma_start(out=outs[w][n, 0].rearrange("(p i) d -> p (i d)", i=TI), in_=osb[(n, w)][:])

        def opose(n, w):
            ni = TI - TS * w
            o = (pso, psq)[w].tile([P, TI, D], F32, name="o%d" % w)
            for i in range(ni):
                nc.tensor.matmul(
                    o[:, i, :], lhsT=qq[(n, w)][:, P * i : P * i + P], rhs=ident[:],
                    is_transpose=w == 0 or i > 0, start=True, stop=True,
                )
            oo[(n, w)] = o

        def rope(n, w):
            ni = TI - TS * w
            o = oo[(n, w)][:, 0:ni, :].unsqueeze(2).to_broadcast([P, ni, 2, D])
            table = tab["t"][:, TI - ni :, :, :].unsqueeze(3).to_broadcast([P, ni, 2, 2, J])
            t = prod.tile([P, 2, ni * D], F32, name="prod%d" % w)
            nc.vector.tensor_tensor(
                out=t[:].rearrange("p c (i h j) -> p i c h j", i=ni, h=2),
                in0=o.rearrange("p i c (h j) -> p i c h j", h=2),
                in1=table,
                op=ALU.mult,
            )
            ab[(n, w)] = t

        def add(n, w, engine):
            if w == 0:
                osb[(n, 0)] = ost.tile([P, TI * D], F32, name="o_sb0")
            t = ab[(n, w)]
            view = "p (f e) -> p f e"
            engine.tensor_tensor(
                out=osb[(n, w)][:, TS * w * D :].rearrange(view, e=2),
                in0=t[:, 0, :].rearrange(view, e=2),
                in1=t[:, 1, :].rearrange(view, e=2)[:, :, ::-1],
                op=ALU.add,
            )

        def rope_s(n):
            osb[(n, 1)] = ost.tile([P, TI * D], F32, name="o_sb1")
            t = prod.tile([P, 2, TS * P], F32, name="prods")
            nc.vector.scalar_tensor_tensor(
                out=t[:], in0=pp[(n, 1)][:, 0 : TS * P].unsqueeze(1).to_broadcast([P, 2, TS * P]),
                scalar=cstb[:, 1:2], in1=tab["f"][:, 0], op0=ALU.add, op1=ALU.mult,
            )
            ab[(n, "s")] = t

        def opose_s(n):
            o = pss.tile([P, TI, D], F32, name="os")
            for i in range(TS):
                for j, moving in ((0, ident), (1, perm)):
                    nc.tensor.matmul(
                        o[:, i, :], lhsT=ab[(n, "s")][:, j, P * i : P * i + P], rhs=moving[:],
                        is_transpose=True, start=j == 0, stop=j == 1,
                    )
            nc.scalar.copy(out=osb[(n, 1)][:, 0 : TS * D], in_=o[:, 0:TS, :].rearrange("p i d -> p (i d)"))

        xpose(0, 0, "scalar")
        xpose(0, 1, "vector")
        sines("f")
        wc = const.tile([P, 2 * D], U32, name="wc", align_bytes=64)
        ws = const.tile([P, 2 * D], U8, name="ws", align_bytes=64)
        nc.vector.quantize_mx(out=wc[:].bitcast(FP8X4), scales=ws[:], in_=wg[:])
        quant(0)
        reduced("t")
        xpose(1, 0, "scalar")
        xpose(1, 1, "scalar")
        setup_b = psq.tile([P, P], F32, name="setup_b", tag="o1")
        nc.tensor.transpose(setup_b[:], brow_f[:], ident[:])
        cstb = const.tile([P, 2], F32, name="cstb")
        nc.vector.tensor_copy(out=cstb[:], in_=setup_b[:, 0:2])
        mx(0)
        biased(0)
        sines("t")
        xpose(2, 0, "scalar")
        opose(0, 1)
        opose(0, 0)
        xpose(2, 1, "scalar")
        rope_s(0)
        quant(1)

        for k in range(NB):
            last = k + 1 == NB
            if not last:
                mx(k + 1)
                biased(k + 1)
            if k + 3 < NB:
                xpose(k + 3, 0, "scalar")
                xpose(k + 3, 1, "scalar")
            if k >= 1:
                rope_s(k)
            rope(k, 1)
            add(k, 1, nc.gpsimd)
            if not last:
                opose(k + 1, 1)
            rope(k, 0)
            if k + 2 < NB:
                quant(k + 2)
            add(k, 0, nc.vector if last else nc.gpsimd)
            if not last:
                opose(k + 1, 0)
            opose_s(k)
            store(k, 1)
            store(k, 0)
